import numpy as np
import ml_dtypes


def mxq(x, axis, fmt="e4m3"):
    dtype, down = {"e4m3": (ml_dtypes.float8_e4m3fn, 7), "e5m2": (ml_dtypes.float8_e5m2, 14)}[fmt]
    v = np.moveaxis(np.asarray(x, np.float32).astype(ml_dtypes.bfloat16).astype(np.float64), axis, -1)
    blocks = v.reshape(v.shape[:-1] + (-1, 32))
    amax = np.abs(blocks).max(-1, keepdims=True)
    byte = np.maximum(np.where(amax > 0, np.frexp(amax)[1] - 1 + 127, 0) - down, 1)
    scale = np.exp2(byte - 127.0)
    codes = (blocks / scale).astype(np.float32).astype(dtype).astype(np.float64)
    return np.moveaxis((codes * scale).reshape(v.shape), -1, axis)


WIDE = False


def mx_kscale(k):
    if not WIDE:
        return np.ones(k)
    levels = np.array([20, -20, 10, -10, 0])
    a = np.random.permutation(np.resize(levels, k // 512 * 4)).reshape(k // 512, 4)
    idx = np.arange(k)
    return np.exp2(a[idx // 512, idx % 128 // 32])


BF16 = ml_dtypes.bfloat16


def bf(x):
    return np.asarray(x, np.float32).astype(BF16)


def f64(x):
    return np.asarray(x).astype(np.float64)


N, K, H = 2048, 2, 256


def sigmoid(v):
    return 1.0 / (1.0 + np.exp(-v))


def setup_inputs():
    t = mx_kscale(4 * H)[:H]
    t2 = np.concatenate([t, t])
    t3 = np.concatenate([t, t, t])
    w = 1.0 / np.sqrt(H * (K + 2))
    mh = f64(bf(np.random.standard_normal((N, K, H))))
    tie = mh[:, 0, :] == mh[:, 1, :]
    mh[:, 1, :] = np.where(tie, mh[:, 1, :] - 0.5, mh[:, 1, :])
    mailbox_h = bf(mh)
    mailbox_c = bf(np.random.standard_normal((N, K, H)) / np.sqrt(K))
    wiou0 = bf(np.random.standard_normal((3 * H, 2 * H)) * w)
    b_iou = bf(np.random.standard_normal((1, 3 * H)) * 0.1)
    wf0 = bf(np.random.standard_normal((H, 2 * H)) * w)
    U_f_b = bf(np.random.standard_normal(H) * 0.1)
    g = bf(np.random.standard_normal((N, 2 * H)) * np.exp2(np.random.randint(-12, 1, (N, 1))) * 8.0 * t2)
    a = f64(mailbox_h)
    hc = np.concatenate([a.sum(axis=1), a.max(axis=1)], axis=1)
    f = sigmoid(hc @ f64(wf0).T + f64(U_f_b))
    iou = hc @ f64(wiou0).T + f64(b_iou)
    zi, zo, zu = np.split(iou, 3, axis=1)
    c = sigmoid(zi) * np.tanh(zu) + f * f64(mailbox_c).sum(axis=1)
    return {"mailbox_h": mailbox_h,
            "mailbox_c": mailbox_c,
            "U_iou_w": bf(f64(wiou0) / t3[:, None]),
            "b_iou": b_iou,
            "U_f_w": bf(f64(wf0) / t[:, None]),
            "U_f_b": U_f_b,
            "iou": np.asarray(iou, np.float32),
            "f": np.asarray(f, np.float32),
            "c": np.asarray(c, np.float32),
            "grad_out": g}


def reference(mailbox_h, mailbox_c, U_iou_w, b_iou, U_f_w, U_f_b, iou, f, c, grad_out):
    mh = f64(mailbox_h)
    mcs = f64(mailbox_c).sum(axis=1)
    g = f64(grad_out)
    gh, gc = g[:, :H], g[:, H:]
    zi, zo, zu = np.split(f64(iou), 3, axis=1)
    si, so, tu = sigmoid(zi), sigmoid(zo), np.tanh(zu)
    tc = np.tanh(f64(c))
    ff = f64(f)
    dc = gc + gh * so * (1.0 - tc * tc)
    di = dc * tu * si * (1.0 - si)
    do = gh * tc * so * (1.0 - so)
    du = dc * si * (1.0 - tu * tu)
    df = dc * mcs * ff * (1.0 - ff)
    dz = np.concatenate([di, do, du, df], axis=1)
    wall = np.concatenate([f64(U_iou_w), f64(U_f_w)], axis=0)
    dhc = mxq(dz, 1, "e5m2") @ mxq(wall, 0, "e4m3")
    hit = np.where(mh == mh.max(axis=1, keepdims=True), 1.0, 0.0)
    share = hit / hit.sum(axis=1, keepdims=True)
    return dhc[:, None, :H] + dhc[:, None, H:] * share

@@ -1,0 +1,258 @@
+from contextlib import ExitStack
+
+import concourse.mybir as mybir
+from concourse.masks import make_identity
+
+F32 = mybir.dt.float32
+BF16 = mybir.dt.bfloat16
+U32 = mybir.dt.uint32
+U8 = mybir.dt.uint8
+E4M3X4 = mybir.dt.float8_e4m3fn_x4
+E5M2X4 = mybir.dt.float8_e5m2_x4
+ALU = mybir.AluOpType
+ACT = mybir.ActivationFunctionType
+
+P = 128
+PACK = 4
+NODES = 2048
+H = 256
+K = 4 * H
+N_OUT = 2 * H
+PASSES = K // (P * PACK)
+K_BLOCKS = K // P
+GROUPS = NODES // P
+GROUPS_PER_CHUNK = 2
+CHUNKS = GROUPS // GROUPS_PER_CHUNK
+LOADS_AHEAD = 3
+
+FLOPS = 2 * NODES * K * N_OUT
+
+
+def tile_treelstmcellv2_t_v_kernel(
+    tc, mailbox_h, mailbox_c, U_iou_w, b_iou, U_f_w, U_f_b, iou, f, c, grad_out, out
+):
+    nc = tc.nc
+    T = GROUPS_PER_CHUNK
+
+    iou_v = iou.rearrange("(p s) k -> p s k", s=GROUPS)
+    f_v = f.rearrange("(p s) j -> p s j", s=GROUPS)
+    c_v = c.rearrange("(p s) j -> p s j", s=GROUPS)
+    g_v = grad_out.rearrange("(p s) k -> p s k", s=GROUPS)
+    mh_v = mailbox_h.rearrange("(p s) k j -> p s k j", s=GROUPS)
+    mc_v = mailbox_c.rearrange("(p s) k j -> p s k j", s=GROUPS)
+    out_v = out.rearrange("(p s) k j -> p s k j", s=GROUPS)
+
+    with ExitStack() as ctx:
+        const = ctx.enter_context(tc.tile_pool(name="const", bufs=1))
+        loads = ctx.enter_context(tc.tile_pool(name="loads", bufs=LOADS_AHEAD))
+        acts = ctx.enter_context(tc.tile_pool(name="acts", bufs=2))
+        signs = ctx.enter_context(tc.tile_pool(name="signs", bufs=3))
+        work = ctx.enter_context(tc.tile_pool(name="work", bufs=2))
+        mx = ctx.enter_context(tc.tile_pool(name="mx", bufs=2))
+        results = ctx.enter_context(tc.tile_pool(name="results", bufs=2))
+        psum_t = ctx.enter_context(tc.psum_pool(name="psum_t", bufs=4))
+        psum_o = ctx.enter_context(tc.psum_pool(name="psum_o", bufs=4))
+
+        w_rows = const.tile([P, K_BLOCKS, N_OUT], BF16, name="w_rows")
+        iou_w_v = U_iou_w.rearrange("(a p) n -> p a n", p=P)
+        f_w_v = U_f_w.rearrange("(a p) n -> p a n", p=P)
+        nc.sync.dma_start(out=w_rows[:, 0:4, :], in_=iou_w_v[:, 0:4, :])
+        nc.sync.dma_start(out=w_rows[:, 4:6, :], in_=iou_w_v[:, 4:6, :])
+        nc.sync.dma_start(out=w_rows[:, 6:8, :], in_=f_w_v)
+
+        def load(j):
+            s = slice(j * T, (j + 1) * T)
+            g_sb = loads.tile([P, T, 2 * H], BF16, name="g_sb")
+            nc.sync.dma_start(out=g_sb[:], in_=g_v[:, s, :])
+            iou_sb = loads.tile([P, T, 3 * H], F32, name="iou_sb")
+            nc.sync.dma_start(out=iou_sb[:], in_=iou_v[:, s, :])
+            c_sb = loads.tile([P, T, H], F32, name="c_sb")
+            nc.sync.dma_start(out=c_sb[:], in_=c_v[:, s, :])
+            mc_sb = loads.tile([P, T, 2, H], BF16, name="mc_sb")
+            nc.sync.dma_start(out=mc_sb[:], in_=mc_v[:, s, :, :])
+            f_sb = loads.tile([P, T, H], F32, name="f_sb")
+            nc.sync.dma_start(out=f_sb[:], in_=f_v[:, s, :])
+            mh_sb = loads.tile([P, T, 2, H], BF16, name="mh_sb")
+            nc.sync.dma_start(out=mh_sb[:], in_=mh_v[:, s, :, :])
+            return {"g": g_sb, "iou": iou_sb, "c": c_sb, "mc": mc_sb, "f": f_sb, "mh": mh_sb}
+
+        inputs = {}
+        for j in range(LOADS_AHEAD):
+            inputs[j] = load(j)
+
+        ident = const.tile([P, P], BF16, name="ident")
+        make_identity(nc, ident[:])
+        neg_half = const.tile([P, 1], F32, name="neg_half")
+        nc.vector.memset(neg_half[:], -0.5)
+
+        w_grouped = const.tile([P, PASSES, N_OUT, PACK], BF16, name="w_grouped", align_bytes=64)
+        w_codes = const.tile([P, PASSES, N_OUT], U32, name="w_codes", align_bytes=64)
+        w_scales = const.tile([P, PASSES, N_OUT], U8, name="w_scales", align_bytes=64)
+        for g in range(PASSES):
+            nc.vector.tensor_copy(
+                out=w_grouped[:, g],
+                in_=w_rows[:, PACK * g : PACK * (g + 1), :].rearrange("p u n -> p n u"),
+            )
+        for g in range(PASSES):
+            nc.vector.quantize_mx(
+                out=w_codes[:, g, :].bitcast(E4M3X4),
+                scales=w_scales[:, g, :],
+                in_=w_grouped[:, g].rearrange("p n u -> p (n u)"),
+            )
+
+        def activations(j):
+            x = inputs[j]
+            sig = acts.tile([P, T, 2 * H], F32, name="sig")
+            nc.scalar.activation(out=sig[:], in_=x["iou"][:, :, 0 : 2 * H], func=ACT.Sigmoid)
+            th = acts.tile([P, 2, T, H], F32, name="th")
+            nc.scalar.activation(out=th[:, 1], in_=x["c"][:], func=ACT.Tanh)
+            nc.scalar.activation(out=th[:, 0], in_=x["iou"][:, :, 2 * H : 3 * H], func=ACT.Tanh)
+            th2 = acts.tile([P, 2, T, H], F32, name="th2")
+            nc.scalar.activation(out=th2[:], in_=th[:], func=ACT.Square)
+            fc2 = acts.tile([P, T, H], F32, name="fc2")
+            nc.scalar.activation(out=fc2[:], in_=x["f"][:], func=ACT.Square, bias=neg_half[:, 0:1])
+            return {"sig": sig, "th": th, "th2": th2, "fc2": fc2}
+
+        def gate_gradients(j):
+            x = inputs[j]
+            a = functions[j]
+            gh = x["g"][:, :, 0:H]
+            gc = x["g"][:, :, H : 2 * H]
+            s_i = a["sig"][:, :, 0:H]
+            s_o = a["sig"][:, :, H : 2 * H]
+            t_u = a["th"][:, 0]
+            t_c = a["th"][:, 1]
+            t_u2 = a["th2"][:, 0]
+            t_c2 = a["th2"][:, 1]
+
+            diff = signs.tile([P, T, H], BF16, name="diff")
+            nc.vector.tensor_tensor(
+                out=diff[:], in0=x["mh"][:, :, 0, :], in1=x["mh"][:, :, 1, :], op=ALU.subtract
+            )
+            dz = mx.tile([P, T, K], BF16, name="dz")
+            q = work.tile([P, T, H], F32, name="q")
+            nc.vector.tensor_tensor(out=q[:], in0=gh, in1=s_o, op=ALU.mult)
+            e_o = work.tile([P, T, H], F32, name="e_o")
+            nc.vector.scalar_tensor_tensor(
+                out=e_o[:], in0=s_o, scalar=1.0, in1=t_c, op0=ALU.subtract, op1=ALU.mult
+            )
+            r = work.tile([P, T, H], F32, name="r")
+            nc.vector.scalar_tensor_tensor(
+                out=r[:], in0=t_c2, scalar=1.0, in1=q[:], op0=ALU.subtract, op1=ALU.mult
+            )
+            mcs = work.tile([P, T, H], F32, name="mcs")
+            nc.vector.tensor_tensor(
+                out=mcs[:], in0=x["mc"][:, :, 0, :], in1=x["mc"][:, :, 1, :], op=ALU.add
+            )
+            dc_neg = work.tile([P, T, H], F32, name="dc_neg")
+            nc.vector.tensor_tensor(out=dc_neg[:], in0=r[:], in1=gc, op=ALU.subtract)
+            nc.vector.scalar_tensor_tensor(
+                out=dz[:, :, H : 2 * H], in0=e_o[:], scalar=-1.0, in1=q[:], op0=ALU.mult, op1=ALU.mult
+            )
+            e_i = work.tile([P, T, H], F32, name="e_i")
+            nc.vector.scalar_tensor_tensor(
+                out=e_i[:], in0=s_i, scalar=1.0, in1=t_u, op0=ALU.subtract, op1=ALU.mult
+            )
+            p = work.tile([P, T, H], F32, name="p")
+            nc.vector.tensor_tensor(out=p[:], in0=dc_neg[:], in1=s_i, op=ALU.mult)
+            g_f = work.tile([P, T, H], F32, name="g_f")
+            nc.vector.scalar_tensor_tensor(
+                out=g_f[:], in0=a["fc2"][:], scalar=0.25, in1=mcs[:], op0=ALU.subtract, op1=ALU.mult
+            )
+            nc.vector.tensor_tensor(out=dz[:, :, 0:H], in0=e_i[:], in1=p[:], op=ALU.mult)
+            nc.vector.tensor_tensor(
+                out=dz[:, :, 3 * H : 4 * H], in0=g_f[:], in1=dc_neg[:], op=ALU.mult
+            )
+            nc.vector.scalar_tensor_tensor(
+                out=dz[:, :, 2 * H : 3 * H], in0=t_u2, scalar=1.0, in1=p[:], op0=ALU.subtract, op1=ALU.mult
+            )
+            return {"dz": dz, "diff": diff}
+
+        def child_signs(j):
+            diff = gradients[j]["diff"]
+            sgn = signs.tile([P, T, 2, H], BF16, name="sgn")
+            nc.scalar.activation(out=sgn[:, :, 0, :], in_=diff[:], func=ACT.Sign)
+            nc.scalar.activation(out=sgn[:, :, 1, :], in_=diff[:], func=ACT.Sign, scale=-1.0)
+            return sgn
+
+        def transpose_dz(j):
+            dz = gradients[j]["dz"]
+            grouped = mx.tile([P, T * K], BF16, name="grouped", align_bytes=64)
+            for t in range(T):
+                dz_t = psum_t.tile([P, K_BLOCKS, P], BF16, name="dz_t")
+                for b in range(K_BLOCKS):
+                    nc.tensor.transpose(dz_t[:, b, :], dz[:, t, b * P : (b + 1) * P], ident[:])
+                nc.scalar.copy(
+                    out=grouped[:, t * K : (t + 1) * K].rearrange(
+                        "p (g r u) -> p g r u", g=PASSES, u=PACK
+                    ),
+                    in_=dz_t[:].rearrange("p (g u) r -> p g r u", u=PACK),
+                )
+            return grouped
+
+        def quantise_and_multiply(j):
+            codes = mx.tile([P, T * PASSES * P], U32, name="codes", align_bytes=64)
+            scales = mx.tile([P, T * PASSES * P], U8, name="scales", align_bytes=64)
+            nc.vector.quantize_mx(
+                out=codes[:].bitcast(E5M2X4), scales=scales[:], in_=grouped_dz[j][:]
+            )
+            products = []
+            for t in range(T):
+                dhc = psum_o.tile([P, N_OUT], F32, name="dhc")
+                for g in range(PASSES):
+                    nodes = slice((t * PASSES + g) * P, (t * PASSES + g + 1) * P)
+                    nc.tensor.matmul_mx(
+                        out=dhc[:],
+                        lhsT=codes[:, nodes].bitcast(E5M2X4),
+                        lhsT_scale=scales[:, nodes],
+                        rhs=w_codes[:, g, :].bitcast(E4M3X4),
+                        rhs_scale=w_scales[:, g, :],
+                        start=(g == 0),
+                        stop=(g == PASSES - 1),
+                    )
+                products.append(dhc)
+            return products
+
+        def finish(j):
+            sgn = sign_of[j]
+            part = results.tile([P, T, 2, H], F32, name="part")
+            o_sb = results.tile([P, T, 2, H], F32, name="o_sb")
+            for t in range(T):
+                nc.vector.scalar_tensor_tensor(
+                    out=part[:, t],
+                    in0=sgn[:, t],
+                    scalar=1.0,
+                    in1=dhc_of[j][t][:, H : 2 * H].unsqueeze(1).to_broadcast([P, 2, H]),
+                    op0=ALU.add,
+                    op1=ALU.mult,
+                )
+            for t in range(T):
+                nc.vector.scalar_tensor_tensor(
+                    out=o_sb[:, t],
+                    in0=part[:, t],
+                    scalar=0.5,
+                    in1=dhc_of[j][t][:, 0:H].unsqueeze(1).to_broadcast([P, 2, H]),
+                    op0=ALU.mult,
+                    op1=ALU.add,
+                )
+                nc.sync.dma_start(out=out_v[:, j * T + t], in_=o_sb[:, t])
+
+        functions = {}
+        gradients = {}
+        sign_of = {}
+        grouped_dz = {}
+        dhc_of = {}
+        functions[0] = activations(0)
+        for j in range(CHUNKS + 2):
+            if j + 1 < CHUNKS:
+                functions[j + 1] = activations(j + 1)
+            if j < CHUNKS:
+                gradients[j] = gate_gradients(j)
+                sign_of[j] = child_signs(j)
+                grouped_dz[j] = transpose_dz(j)
+            if j + LOADS_AHEAD < CHUNKS:
+                inputs[j + LOADS_AHEAD] = load(j + LOADS_AHEAD)
+            if 1 <= j <= CHUNKS:
+                dhc_of[j - 1] = quantise_and_multiply(j - 1)
+            if j >= 2:
+                finish(j - 2)

@@ -50,8 +50,8 @@ def tile_treelstmcellv2_t_v_kernel(
         work = ctx.enter_context(tc.tile_pool(name="work", bufs=2))
         mx = ctx.enter_context(tc.tile_pool(name="mx", bufs=2))
         results = ctx.enter_context(tc.tile_pool(name="results", bufs=2))
-        psum_t = ctx.enter_context(tc.psum_pool(name="psum_t", bufs=4))
-        psum_o = ctx.enter_context(tc.psum_pool(name="psum_o", bufs=4))
+        psum_t = ctx.enter_context(tc.psum_pool(name="psum_t", bufs=2))
+        psum_o = ctx.enter_context(tc.psum_pool(name="psum_o", bufs=3))
 
         w_rows = const.tile([P, K_BLOCKS, N_OUT], BF16, name="w_rows")
         iou_w_v = U_iou_w.rearrange("(a p) n -> p a n", p=P)
@@ -86,8 +86,8 @@ def tile_treelstmcellv2_t_v_kernel(
         nc.vector.memset(neg_half[:], -0.5)
 
         w_grouped = const.tile([P, PASSES, N_OUT, PACK], BF16, name="w_grouped", align_bytes=64)
-        w_codes = const.tile([P, PASSES, N_OUT], U32, name="w_codes", align_bytes=64)
-        w_scales = const.tile([P, PASSES, N_OUT], U8, name="w_scales", align_bytes=64)
+        w_codes = const.tile([P, PASSES, N_OUT + H], U32, name="w_codes", align_bytes=64)
+        w_scales = const.tile([P, PASSES, N_OUT + H], U8, name="w_scales", align_bytes=64)
         for g in range(PASSES):
             nc.vector.tensor_copy(
                 out=w_grouped[:, g],
@@ -95,9 +95,14 @@ def tile_treelstmcellv2_t_v_kernel(
             )
         for g in range(PASSES):
             nc.vector.quantize_mx(
-                out=w_codes[:, g, :].bitcast(E4M3X4),
-                scales=w_scales[:, g, :],
+                out=w_codes[:, g, 0:N_OUT].bitcast(E4M3X4),
+                scales=w_scales[:, g, 0:N_OUT],
                 in_=w_grouped[:, g].rearrange("p n u -> p (n u)"),
+            )
+            nc.vector.quantize_mx(
+                out=w_codes[:, g, N_OUT : N_OUT + H].bitcast(E4M3X4),
+                scales=w_scales[:, g, N_OUT : N_OUT + H],
+                in_=w_grouped[:, g, 0:H, :].rearrange("p n u -> p (n u)"),
             )
 
         def activations(j):
@@ -168,11 +173,9 @@ def tile_treelstmcellv2_t_v_kernel(
             )
             return {"dz": dz, "diff": diff}
 
-        def child_signs(j):
-            diff = gradients[j]["diff"]
-            sgn = signs.tile([P, T, 2, H], BF16, name="sgn")
-            nc.scalar.activation(out=sgn[:, :, 0, :], in_=diff[:], func=ACT.Sign)
-            nc.scalar.activation(out=sgn[:, :, 1, :], in_=diff[:], func=ACT.Sign, scale=-1.0)
+        def child_sign(j):
+            sgn = signs.tile([P, T, H], BF16, name="sgn")
+            nc.scalar.activation(out=sgn[:], in_=gradients[j]["diff"][:], func=ACT.Sign)
             return sgn
 
         def transpose_dz(j):
@@ -190,69 +193,96 @@ def tile_treelstmcellv2_t_v_kernel(
                 )
             return grouped
 
-        def quantise_and_multiply(j):
+        def quantise(j):
             codes = mx.tile([P, T * PASSES * P], U32, name="codes", align_bytes=64)
             scales = mx.tile([P, T * PASSES * P], U8, name="scales", align_bytes=64)
             nc.vector.quantize_mx(
                 out=codes[:].bitcast(E5M2X4), scales=scales[:], in_=grouped_dz[j][:]
             )
-            products = []
-            for t in range(T):
-                dhc = psum_o.tile([P, N_OUT], F32, name="dhc")
-                for g in range(PASSES):
-                    nodes = slice((t * PASSES + g) * P, (t * PASSES + g + 1) * P)
-                    nc.tensor.matmul_mx(
-                        out=dhc[:],
-                        lhsT=codes[:, nodes].bitcast(E5M2X4),
-                        lhsT_scale=scales[:, nodes],
-                        rhs=w_codes[:, g, :].bitcast(E4M3X4),
-                        rhs_scale=w_scales[:, g, :],
-                        start=(g == 0),
-                        stop=(g == PASSES - 1),
-                    )
-                products.append(dhc)
-            return products
+            return {"codes": codes, "scales": scales}
 
-        def finish(j):
-            sgn = sign_of[j]
-            part = results.tile([P, T, 2, H], F32, name="part")
-            o_sb = results.tile([P, T, 2, H], F32, name="o_sb")
+        def multiply(j, t):
+            codes = quantised[j]["codes"]
+            scales = quantised[j]["scales"]
+            dhc = psum_o.tile([P, N_OUT], F32, name="dhc")
+            both = psum_o.tile([P, N_OUT], F32, name="both")
+
+            def one_pass(acc, g, w_from, start, stop):
+                nodes = slice((t * PASSES + g) * P, (t * PASSES + g + 1) * P)
+                nc.tensor.matmul_mx(
+                    out=acc[:],
+                    lhsT=codes[:, nodes].bitcast(E5M2X4),
+                    lhsT_scale=scales[:, nodes],
+                    rhs=w_codes[:, g, w_from : w_from + N_OUT].bitcast(E4M3X4),
+                    rhs_scale=w_scales[:, g, w_from : w_from + N_OUT],
+                    start=start,
+                    stop=stop,
+                )
+
+            for g in range(PASSES):
+                first = g == 0
+                last = g == PASSES - 1
+                one_pass(dhc, g, 0, first, last)
+                one_pass(both, g, 0, first, False)
+                one_pass(both, g, H, False, last)
+            return {"dhc": dhc, "both": both}
+
+        def shared_part(j):
+            part = results.tile([P, T, H], F32, name="part")
             for t in range(T):
                 nc.vector.scalar_tensor_tensor(
                     out=part[:, t],
-                    in0=sgn[:, t],
+                    in0=sign_of[j][:, t],
                     scalar=1.0,
-                    in1=dhc_of[j][t][:, H : 2 * H].unsqueeze(1).to_broadcast([P, 2, H]),
+                    in1=products[j, t]["dhc"][:, H : 2 * H],
                     op0=ALU.add,
                     op1=ALU.mult,
                 )
-            for t in range(T):
-                nc.vector.scalar_tensor_tensor(
-                    out=o_sb[:, t],
-                    in0=part[:, t],
-                    scalar=0.5,
-                    in1=dhc_of[j][t][:, 0:H].unsqueeze(1).to_broadcast([P, 2, H]),
-                    op0=ALU.mult,
-                    op1=ALU.add,
-                )
-                nc.sync.dma_start(out=out_v[:, j * T + t], in_=o_sb[:, t])
+            return part
+
+        def finish(j, t):
+            o_sb = results.tile([P, 2, H], F32, name="o_sb")
+            nc.vector.scalar_tensor_tensor(
+                out=o_sb[:, 0, :],
+                in0=part_of[j][:, t],
+                scalar=0.5,
+                in1=products[j, t]["dhc"][:, 0:H],
+                op0=ALU.mult,
+                op1=ALU.add,
+            )
+            nc.vector.scalar_tensor_tensor(
+                out=o_sb[:, 1, :],
+                in0=part_of[j][:, t],
+                scalar=-0.5,
+                in1=products[j, t]["both"][:, 0:H],
+                op0=ALU.mult,
+                op1=ALU.add,
+            )
+            nc.sync.dma_start(out=out_v[:, j * T + t], in_=o_sb[:])
 
         functions = {}
         gradients = {}
         sign_of = {}
         grouped_dz = {}
-        dhc_of = {}
+        quantised = {}
+        products = {}
+        part_of = {}
         functions[0] = activations(0)
         for j in range(CHUNKS + 2):
             if j + 1 < CHUNKS:
                 functions[j + 1] = activations(j + 1)
             if j < CHUNKS:
                 gradients[j] = gate_gradients(j)
-                sign_of[j] = child_signs(j)
+                sign_of[j] = child_sign(j)
                 grouped_dz[j] = transpose_dz(j)
             if j + LOADS_AHEAD < CHUNKS:
                 inputs[j + LOADS_AHEAD] = load(j + LOADS_AHEAD)
             if 1 <= j <= CHUNKS:
-                dhc_of[j - 1] = quantise_and_multiply(j - 1)
+                quantised[j - 1] = quantise(j - 1)
             if j >= 2:
-                finish(j - 2)
+                part_of[j - 2] = shared_part(j - 2)
+            for t in range(T):
+                if 1 <= j <= CHUNKS:
+                    products[j - 1, t] = multiply(j - 1, t)
+                if j >= 2:
+                    finish(j - 2, t)

@@ -22,8 +22,10 @@ PASSES = K // (P * PACK)
 K_BLOCKS = K // P
 GROUPS = NODES // P
 GROUPS_PER_CHUNK = 2
-CHUNKS = GROUPS // GROUPS_PER_CHUNK
+CHUNK_SIZES = [GROUPS_PER_CHUNK] * (GROUPS // GROUPS_PER_CHUNK - 1) + [1] * GROUPS_PER_CHUNK
+CHUNKS = len(CHUNK_SIZES)
 LOADS_AHEAD = 3
+FIRST_GPSIMD_CHUNK = 3
 
 FLOPS = 2 * NODES * K * N_OUT
 
@@ -32,7 +34,7 @@ def tile_treelstmcellv2_t_v_kernel(
     tc, mailbox_h, mailbox_c, U_iou_w, b_iou, U_f_w, U_f_b, iou, f, c, grad_out, out
 ):
     nc = tc.nc
-    T = GROUPS_PER_CHUNK
+    first_group = [sum(CHUNK_SIZES[:j]) for j in range(CHUNKS)]
 
     iou_v = iou.rearrange("(p s) k -> p s k", s=GROUPS)
     f_v = f.rearrange("(p s) j -> p s j", s=GROUPS)
@@ -43,10 +45,12 @@ def tile_treelstmcellv2_t_v_kernel(
     out_v = out.rearrange("(p s) k j -> p s k j", s=GROUPS)
 
     with ExitStack() as ctx:
+        ctx.enter_context(tc.manual_schedule())
         const = ctx.enter_context(tc.tile_pool(name="const", bufs=1))
         loads = ctx.enter_context(tc.tile_pool(name="loads", bufs=LOADS_AHEAD))
         acts = ctx.enter_context(tc.tile_pool(name="acts", bufs=2))
         signs = ctx.enter_context(tc.tile_pool(name="signs", bufs=3))
+        sums = ctx.enter_context(tc.tile_pool(name="sums", bufs=1))
         work = ctx.enter_context(tc.tile_pool(name="work", bufs=2))
         mx = ctx.enter_context(tc.tile_pool(name="mx", bufs=2))
         results = ctx.enter_context(tc.tile_pool(name="results", bufs=2))
@@ -61,18 +65,19 @@ def tile_treelstmcellv2_t_v_kernel(
         nc.sync.dma_start(out=w_rows[:, 6:8, :], in_=f_w_v)
 
         def load(j):
-            s = slice(j * T, (j + 1) * T)
-            g_sb = loads.tile([P, T, 2 * H], BF16, name="g_sb")
-            nc.sync.dma_start(out=g_sb[:], in_=g_v[:, s, :])
-            iou_sb = loads.tile([P, T, 3 * H], F32, name="iou_sb")
+            n = CHUNK_SIZES[j]
+            s = slice(first_group[j], first_group[j] + n)
+            iou_sb = loads.tile([P, n, 3 * H], F32, name="iou_sb")
             nc.sync.dma_start(out=iou_sb[:], in_=iou_v[:, s, :])
-            c_sb = loads.tile([P, T, H], F32, name="c_sb")
+            g_sb = loads.tile([P, n, 2 * H], BF16, name="g_sb")
+            nc.sync.dma_start(out=g_sb[:], in_=g_v[:, s, :])
+            c_sb = loads.tile([P, n, H], F32, name="c_sb")
             nc.sync.dma_start(out=c_sb[:], in_=c_v[:, s, :])
-            mc_sb = loads.tile([P, T, 2, H], BF16, name="mc_sb")
+            mc_sb = loads.tile([P, n, 2, H], BF16, name="mc_sb")
             nc.sync.dma_start(out=mc_sb[:], in_=mc_v[:, s, :, :])
-            f_sb = loads.tile([P, T, H], F32, name="f_sb")
+            f_sb = loads.tile([P, n, H], F32, name="f_sb")
             nc.sync.dma_start(out=f_sb[:], in_=f_v[:, s, :])
-            mh_sb = loads.tile([P, T, 2, H], BF16, name="mh_sb")
+            mh_sb = loads.tile([P, n, 2, H], BF16, name="mh_sb")
             nc.sync.dma_start(out=mh_sb[:], in_=mh_v[:, s, :, :])
             return {"g": g_sb, "iou": iou_sb, "c": c_sb, "mc": mc_sb, "f": f_sb, "mh": mh_sb}
 
@@ -90,8 +95,8 @@ def tile_treelstmcellv2_t_v_kernel(
         w_scales = const.tile([P, PASSES, N_OUT + H], U8, name="w_scales", align_bytes=64)
         for g in range(PASSES):
             nc.vector.tensor_copy(
-                out=w_grouped[:, g],
-                in_=w_rows[:, PACK * g : PACK * (g + 1), :].rearrange("p u n -> p n u"),
+                out=w_grouped[:, g].rearrange("p (c i) u -> p c u i", i=4),
+                in_=w_rows[:, PACK * g : PACK * (g + 1), :].rearrange("p u (c i) -> p c u i", i=4),
             )
         for g in range(PASSES):
             nc.vector.quantize_mx(
@@ -106,19 +111,27 @@ def tile_treelstmcellv2_t_v_kernel(
             )
 
         def activations(j):
+            n = CHUNK_SIZES[j]
             x = inputs[j]
-            sig = acts.tile([P, T, 2 * H], F32, name="sig")
+            sig = acts.tile([P, n, 2 * H], F32, name="sig")
             nc.scalar.activation(out=sig[:], in_=x["iou"][:, :, 0 : 2 * H], func=ACT.Sigmoid)
-            th = acts.tile([P, 2, T, H], F32, name="th")
+            th = acts.tile([P, 2, n, H], F32, name="th")
             nc.scalar.activation(out=th[:, 1], in_=x["c"][:], func=ACT.Tanh)
             nc.scalar.activation(out=th[:, 0], in_=x["iou"][:, :, 2 * H : 3 * H], func=ACT.Tanh)
-            th2 = acts.tile([P, 2, T, H], F32, name="th2")
+            th2 = acts.tile([P, 2, n, H], F32, name="th2")
             nc.scalar.activation(out=th2[:], in_=th[:], func=ACT.Square)
-            fc2 = acts.tile([P, T, H], F32, name="fc2")
+            fc2 = acts.tile([P, n, H], F32, name="fc2")
             nc.scalar.activation(out=fc2[:], in_=x["f"][:], func=ACT.Square, bias=neg_half[:, 0:1])
             return {"sig": sig, "th": th, "th2": th2, "fc2": fc2}
 
+        def children_sum(engine, j):
+            mc = inputs[j]["mc"]
+            mcs = sums.tile([P, CHUNK_SIZES[j], H], F32, name="mcs")
+            engine.tensor_tensor(out=mcs[:], in0=mc[:, :, 0, :], in1=mc[:, :, 1, :], op=ALU.add)
+            return mcs
+
         def gate_gradients(j):
+            n = CHUNK_SIZES[j]
             x = inputs[j]
             a = functions[j]
             gh = x["g"][:, :, 0:H]
@@ -130,58 +143,57 @@ def tile_treelstmcellv2_t_v_kernel(
             t_u2 = a["th2"][:, 0]
             t_c2 = a["th2"][:, 1]
 
-            diff = signs.tile([P, T, H], BF16, name="diff")
-            nc.vector.tensor_tensor(
-                out=diff[:], in0=x["mh"][:, :, 0, :], in1=x["mh"][:, :, 1, :], op=ALU.subtract
-            )
-            dz = mx.tile([P, T, K], BF16, name="dz")
-            q = work.tile([P, T, H], F32, name="q")
+            dz = mx.tile([P, n, K], BF16, name="dz")
+            q = work.tile([P, n, H], F32, name="q")
             nc.vector.tensor_tensor(out=q[:], in0=gh, in1=s_o, op=ALU.mult)
-            e_o = work.tile([P, T, H], F32, name="e_o")
+            e_o = work.tile([P, n, H], F32, name="e_o")
             nc.vector.scalar_tensor_tensor(
                 out=e_o[:], in0=s_o, scalar=1.0, in1=t_c, op0=ALU.subtract, op1=ALU.mult
             )
-            r = work.tile([P, T, H], F32, name="r")
-            nc.vector.scalar_tensor_tensor(
-                out=r[:], in0=t_c2, scalar=1.0, in1=q[:], op0=ALU.subtract, op1=ALU.mult
-            )
-            mcs = work.tile([P, T, H], F32, name="mcs")
-            nc.vector.tensor_tensor(
-                out=mcs[:], in0=x["mc"][:, :, 0, :], in1=x["mc"][:, :, 1, :], op=ALU.add
-            )
-            dc_neg = work.tile([P, T, H], F32, name="dc_neg")
-            nc.vector.tensor_tensor(out=dc_neg[:], in0=r[:], in1=gc, op=ALU.subtract)
-            nc.vector.scalar_tensor_tensor(
-                out=dz[:, :, H : 2 * H], in0=e_o[:], scalar=-1.0, in1=q[:], op0=ALU.mult, op1=ALU.mult
-            )
-            e_i = work.tile([P, T, H], F32, name="e_i")
+            e_i = work.tile([P, n, H], F32, name="e_i")
             nc.vector.scalar_tensor_tensor(
                 out=e_i[:], in0=s_i, scalar=1.0, in1=t_u, op0=ALU.subtract, op1=ALU.mult
             )
-            p = work.tile([P, T, H], F32, name="p")
-            nc.vector.tensor_tensor(out=p[:], in0=dc_neg[:], in1=s_i, op=ALU.mult)
-            g_f = work.tile([P, T, H], F32, name="g_f")
+            r = work.tile([P, n, H], F32, name="r")
             nc.vector.scalar_tensor_tensor(
-                out=g_f[:], in0=a["fc2"][:], scalar=0.25, in1=mcs[:], op0=ALU.subtract, op1=ALU.mult
+                out=r[:], in0=t_c2, scalar=1.0, in1=q[:], op0=ALU.subtract, op1=ALU.mult
+            )
+            if j < FIRST_GPSIMD_CHUNK:
+                mcs_of[j] = children_sum(nc.vector, j)
+            nc.vector.scalar_tensor_tensor(
+                out=dz[:, :, H : 2 * H], in0=e_o[:], scalar=-1.0, in1=q[:], op0=ALU.mult, op1=ALU.mult
+            )
+            dc_neg = work.tile([P, n, H], F32, name="dc_neg")
+            nc.vector.tensor_tensor(out=dc_neg[:], in0=r[:], in1=gc, op=ALU.subtract)
+            diff = signs.tile([P, n, H], BF16, name="diff")
+            nc.vector.tensor_tensor(
+                out=diff[:], in0=x["mh"][:, :, 0, :], in1=x["mh"][:, :, 1, :], op=ALU.subtract
+            )
+            p = work.tile([P, n, H], F32, name="p")
+            nc.vector.tensor_tensor(out=p[:], in0=dc_neg[:], in1=s_i, op=ALU.mult)
+            g_f = work.tile([P, n, H], F32, name="g_f")
+            nc.vector.scalar_tensor_tensor(
+                out=g_f[:], in0=a["fc2"][:], scalar=0.25, in1=mcs_of[j][:], op0=ALU.subtract, op1=ALU.mult
             )
             nc.vector.tensor_tensor(out=dz[:, :, 0:H], in0=e_i[:], in1=p[:], op=ALU.mult)
-            nc.vector.tensor_tensor(
-                out=dz[:, :, 3 * H : 4 * H], in0=g_f[:], in1=dc_neg[:], op=ALU.mult
-            )
             nc.vector.scalar_tensor_tensor(
                 out=dz[:, :, 2 * H : 3 * H], in0=t_u2, scalar=1.0, in1=p[:], op0=ALU.subtract, op1=ALU.mult
+            )
+            nc.vector.tensor_tensor(
+                out=dz[:, :, 3 * H : 4 * H], in0=g_f[:], in1=dc_neg[:], op=ALU.mult
             )
             return {"dz": dz, "diff": diff}
 
         def child_sign(j):
-            sgn = signs.tile([P, T, H], BF16, name="sgn")
+            sgn = signs.tile([P, CHUNK_SIZES[j], H], BF16, name="sgn")
             nc.scalar.activation(out=sgn[:], in_=gradients[j]["diff"][:], func=ACT.Sign)
             return sgn
 
         def transpose_dz(j):
+            n = CHUNK_SIZES[j]
             dz = gradients[j]["dz"]
-            grouped = mx.tile([P, T * K], BF16, name="grouped", align_bytes=64)
-            for t in range(T):
+            grouped = mx.tile([P, n * K], BF16, name="grouped", align_bytes=64)
+            for t in range(n):
                 dz_t = psum_t.tile([P, K_BLOCKS, P], BF16, name="dz_t")
                 for b in range(K_BLOCKS):
                     nc.tensor.transpose(dz_t[:, b, :], dz[:, t, b * P : (b + 1) * P], ident[:])
@@ -194,8 +206,9 @@ def tile_treelstmcellv2_t_v_kernel(
             return grouped
 
         def quantise(j):
-            codes = mx.tile([P, T * PASSES * P], U32, name="codes", align_bytes=64)
-            scales = mx.tile([P, T * PASSES * P], U8, name="scales", align_bytes=64)
+            n = CHUNK_SIZES[j]
+            codes = mx.tile([P, n * PASSES * P], U32, name="codes", align_bytes=64)
+            scales = mx.tile([P, n * PASSES * P], U8, name="scales", align_bytes=64)
             nc.vector.quantize_mx(
                 out=codes[:].bitcast(E5M2X4), scales=scales[:], in_=grouped_dz[j][:]
             )
@@ -228,8 +241,8 @@ def tile_treelstmcellv2_t_v_kernel(
             return {"dhc": dhc, "both": both}
 
         def shared_part(j):
-            part = results.tile([P, T, H], F32, name="part")
-            for t in range(T):
+            part = results.tile([P, CHUNK_SIZES[j], H], F32, name="part")
+            for t in range(CHUNK_SIZES[j]):
                 nc.vector.scalar_tensor_tensor(
                     out=part[:, t],
                     in0=sign_of[j][:, t],
@@ -258,9 +271,10 @@ def tile_treelstmcellv2_t_v_kernel(
                 op0=ALU.mult,
                 op1=ALU.add,
             )
-            nc.sync.dma_start(out=out_v[:, j * T + t], in_=o_sb[:])
+            nc.sync.dma_start(out=out_v[:, first_group[j] + t], in_=o_sb[:])
 
         functions = {}
+        mcs_of = {}
         gradients = {}
         sign_of = {}
         grouped_dz = {}
@@ -277,12 +291,14 @@ def tile_treelstmcellv2_t_v_kernel(
                 grouped_dz[j] = transpose_dz(j)
             if j + LOADS_AHEAD < CHUNKS:
                 inputs[j + LOADS_AHEAD] = load(j + LOADS_AHEAD)
+            if FIRST_GPSIMD_CHUNK <= j + 1 < CHUNKS:
+                mcs_of[j + 1] = children_sum(nc.gpsimd, j + 1)
             if 1 <= j <= CHUNKS:
                 quantised[j - 1] = quantise(j - 1)
             if j >= 2:
                 part_of[j - 2] = shared_part(j - 2)
-            for t in range(T):
-                if 1 <= j <= CHUNKS:
+            for t in range(GROUPS_PER_CHUNK):
+                if 1 <= j <= CHUNKS and t < CHUNK_SIZES[j - 1]:
                     products[j - 1, t] = multiply(j - 1, t)
-                if j >= 2:
+                if j >= 2 and t < CHUNK_SIZES[j - 2]:
                     finish(j - 2, t)

@@ -54,6 +54,7 @@ def tile_treelstmcellv2_t_v_kernel(
         work = ctx.enter_context(tc.tile_pool(name="work", bufs=2))
         mx = ctx.enter_context(tc.tile_pool(name="mx", bufs=2))
         results = ctx.enter_context(tc.tile_pool(name="results", bufs=2))
+        stores = ctx.enter_context(tc.tile_pool(name="stores", bufs=4))
         psum_t = ctx.enter_context(tc.psum_pool(name="psum_t", bufs=2))
         psum_o = ctx.enter_context(tc.psum_pool(name="psum_o", bufs=3))
 
@@ -254,7 +255,7 @@ def tile_treelstmcellv2_t_v_kernel(
             return part
 
         def finish(j, t):
-            o_sb = results.tile([P, 2, H], F32, name="o_sb")
+            o_sb = stores.tile([P, 2, H], F32, name="o_sb")
             nc.vector.scalar_tensor_tensor(
                 out=o_sb[:, 0, :],
                 in0=part_of[j][:, t],

@@ -20,6 +20,8 @@ K = 4 * H
 N_OUT = 2 * H
 PASSES = K // (P * PACK)
 K_BLOCKS = K // P
+IOU_BLOCKS = 3 * H // P
+COPY_RUN = 4
 GROUPS = NODES // P
 GROUPS_PER_CHUNK = 2
 CHUNK_SIZES = [GROUPS_PER_CHUNK] * (GROUPS // GROUPS_PER_CHUNK - 1) + [1] * GROUPS_PER_CHUNK
@@ -36,51 +38,51 @@ def tile_treelstmcellv2_t_v_kernel(
     nc = tc.nc
     first_group = [sum(CHUNK_SIZES[:j]) for j in range(CHUNKS)]
 
-    iou_v = iou.rearrange("(p s) k -> p s k", s=GROUPS)
-    f_v = f.rearrange("(p s) j -> p s j", s=GROUPS)
-    c_v = c.rearrange("(p s) j -> p s j", s=GROUPS)
-    g_v = grad_out.rearrange("(p s) k -> p s k", s=GROUPS)
-    mh_v = mailbox_h.rearrange("(p s) k j -> p s k j", s=GROUPS)
-    mc_v = mailbox_c.rearrange("(p s) k j -> p s k j", s=GROUPS)
-    out_v = out.rearrange("(p s) k j -> p s k j", s=GROUPS)
+    iou_v = iou.rearrange("(p s) z -> p s z", s=GROUPS)
+    f_v = f.rearrange("(p s) h -> p s h", s=GROUPS)
+    c_v = c.rearrange("(p s) h -> p s h", s=GROUPS)
+    grad_v = grad_out.rearrange("(p s) y -> p s y", s=GROUPS)
+    mh_v = mailbox_h.rearrange("(p s) child h -> p s child h", s=GROUPS)
+    mc_v = mailbox_c.rearrange("(p s) child h -> p s child h", s=GROUPS)
+    out_v = out.rearrange("(p s) child h -> p s child h", s=GROUPS)
 
     with ExitStack() as ctx:
         ctx.enter_context(tc.manual_schedule())
         const = ctx.enter_context(tc.tile_pool(name="const", bufs=1))
         loads = ctx.enter_context(tc.tile_pool(name="loads", bufs=LOADS_AHEAD))
         acts = ctx.enter_context(tc.tile_pool(name="acts", bufs=2))
-        signs = ctx.enter_context(tc.tile_pool(name="signs", bufs=3))
-        sums = ctx.enter_context(tc.tile_pool(name="sums", bufs=1))
         work = ctx.enter_context(tc.tile_pool(name="work", bufs=2))
         mx = ctx.enter_context(tc.tile_pool(name="mx", bufs=2))
         results = ctx.enter_context(tc.tile_pool(name="results", bufs=2))
+        signs = ctx.enter_context(tc.tile_pool(name="signs", bufs=3))
+        early = ctx.enter_context(tc.tile_pool(name="early", bufs=1))
         stores = ctx.enter_context(tc.tile_pool(name="stores", bufs=4))
         psum_t = ctx.enter_context(tc.psum_pool(name="psum_t", bufs=2))
         psum_o = ctx.enter_context(tc.psum_pool(name="psum_o", bufs=3))
 
         w_rows = const.tile([P, K_BLOCKS, N_OUT], BF16, name="w_rows")
-        iou_w_v = U_iou_w.rearrange("(a p) n -> p a n", p=P)
-        f_w_v = U_f_w.rearrange("(a p) n -> p a n", p=P)
-        nc.sync.dma_start(out=w_rows[:, 0:4, :], in_=iou_w_v[:, 0:4, :])
-        nc.sync.dma_start(out=w_rows[:, 4:6, :], in_=iou_w_v[:, 4:6, :])
-        nc.sync.dma_start(out=w_rows[:, 6:8, :], in_=f_w_v)
+        iou_w_v = U_iou_w.rearrange("(blk p) n -> p blk n", p=P)
+        f_w_v = U_f_w.rearrange("(blk p) n -> p blk n", p=P)
+        nc.sync.dma_start(out=w_rows[:, 0:PACK, :], in_=iou_w_v[:, 0:PACK, :])
+        nc.sync.dma_start(out=w_rows[:, PACK:IOU_BLOCKS, :], in_=iou_w_v[:, PACK:IOU_BLOCKS, :])
+        nc.sync.dma_start(out=w_rows[:, IOU_BLOCKS:K_BLOCKS, :], in_=f_w_v)
 
         def load(j):
-            n = CHUNK_SIZES[j]
-            s = slice(first_group[j], first_group[j] + n)
-            iou_sb = loads.tile([P, n, 3 * H], F32, name="iou_sb")
-            nc.sync.dma_start(out=iou_sb[:], in_=iou_v[:, s, :])
-            g_sb = loads.tile([P, n, 2 * H], BF16, name="g_sb")
-            nc.sync.dma_start(out=g_sb[:], in_=g_v[:, s, :])
-            c_sb = loads.tile([P, n, H], F32, name="c_sb")
-            nc.sync.dma_start(out=c_sb[:], in_=c_v[:, s, :])
-            mc_sb = loads.tile([P, n, 2, H], BF16, name="mc_sb")
-            nc.sync.dma_start(out=mc_sb[:], in_=mc_v[:, s, :, :])
-            f_sb = loads.tile([P, n, H], F32, name="f_sb")
-            nc.sync.dma_start(out=f_sb[:], in_=f_v[:, s, :])
-            mh_sb = loads.tile([P, n, 2, H], BF16, name="mh_sb")
-            nc.sync.dma_start(out=mh_sb[:], in_=mh_v[:, s, :, :])
-            return {"g": g_sb, "iou": iou_sb, "c": c_sb, "mc": mc_sb, "f": f_sb, "mh": mh_sb}
+            size = CHUNK_SIZES[j]
+            groups = slice(first_group[j], first_group[j] + size)
+            iou_sb = loads.tile([P, size, 3 * H], F32, name="iou_sb")
+            nc.sync.dma_start(out=iou_sb[:], in_=iou_v[:, groups, :])
+            grad_sb = loads.tile([P, size, 2 * H], BF16, name="grad_sb")
+            nc.sync.dma_start(out=grad_sb[:], in_=grad_v[:, groups, :])
+            c_sb = loads.tile([P, size, H], F32, name="c_sb")
+            nc.sync.dma_start(out=c_sb[:], in_=c_v[:, groups, :])
+            mc_sb = loads.tile([P, size, 2, H], BF16, name="mc_sb")
+            nc.sync.dma_start(out=mc_sb[:], in_=mc_v[:, groups, :, :])
+            f_sb = loads.tile([P, size, H], F32, name="f_sb")
+            nc.sync.dma_start(out=f_sb[:], in_=f_v[:, groups, :])
+            mh_sb = loads.tile([P, size, 2, H], BF16, name="mh_sb")
+            nc.sync.dma_start(out=mh_sb[:], in_=mh_v[:, groups, :, :])
+            return {"iou": iou_sb, "grad": grad_sb, "c": c_sb, "mc": mc_sb, "f": f_sb, "mh": mh_sb}
 
         inputs = {}
         for j in range(LOADS_AHEAD):
@@ -96,92 +98,111 @@ def tile_treelstmcellv2_t_v_kernel(
         w_scales = const.tile([P, PASSES, N_OUT + H], U8, name="w_scales", align_bytes=64)
         for g in range(PASSES):
             nc.vector.tensor_copy(
-                out=w_grouped[:, g].rearrange("p (c i) u -> p c u i", i=4),
-                in_=w_rows[:, PACK * g : PACK * (g + 1), :].rearrange("p u (c i) -> p c u i", i=4),
+                out=w_grouped[:, g].rearrange("p (run i) v -> p run v i", i=COPY_RUN),
+                in_=w_rows[:, PACK * g : PACK * (g + 1), :].rearrange(
+                    "p v (run i) -> p run v i", i=COPY_RUN
+                ),
             )
         for g in range(PASSES):
             nc.vector.quantize_mx(
                 out=w_codes[:, g, 0:N_OUT].bitcast(E4M3X4),
                 scales=w_scales[:, g, 0:N_OUT],
-                in_=w_grouped[:, g].rearrange("p n u -> p (n u)"),
+                in_=w_grouped[:, g].rearrange("p n v -> p (n v)"),
             )
             nc.vector.quantize_mx(
                 out=w_codes[:, g, N_OUT : N_OUT + H].bitcast(E4M3X4),
                 scales=w_scales[:, g, N_OUT : N_OUT + H],
-                in_=w_grouped[:, g, 0:H, :].rearrange("p n u -> p (n u)"),
+                in_=w_grouped[:, g, 0:H, :].rearrange("p n v -> p (n v)"),
             )
 
         def activations(j):
-            n = CHUNK_SIZES[j]
+            size = CHUNK_SIZES[j]
             x = inputs[j]
-            sig = acts.tile([P, n, 2 * H], F32, name="sig")
+            sig = acts.tile([P, size, 2 * H], F32, name="sig")
             nc.scalar.activation(out=sig[:], in_=x["iou"][:, :, 0 : 2 * H], func=ACT.Sigmoid)
-            th = acts.tile([P, 2, n, H], F32, name="th")
+            th = acts.tile([P, 2, size, H], F32, name="th")
             nc.scalar.activation(out=th[:, 1], in_=x["c"][:], func=ACT.Tanh)
             nc.scalar.activation(out=th[:, 0], in_=x["iou"][:, :, 2 * H : 3 * H], func=ACT.Tanh)
-            th2 = acts.tile([P, 2, n, H], F32, name="th2")
+            th2 = acts.tile([P, 2, size, H], F32, name="th2")
             nc.scalar.activation(out=th2[:], in_=th[:], func=ACT.Square)
-            fc2 = acts.tile([P, n, H], F32, name="fc2")
+            fc2 = acts.tile([P, size, H], F32, name="fc2")
             nc.scalar.activation(out=fc2[:], in_=x["f"][:], func=ACT.Square, bias=neg_half[:, 0:1])
             return {"sig": sig, "th": th, "th2": th2, "fc2": fc2}
 
-        def children_sum(engine, j):
+        def early_results(engine, j):
+            size = CHUNK_SIZES[j]
             mc = inputs[j]["mc"]
-            mcs = sums.tile([P, CHUNK_SIZES[j], H], F32, name="mcs")
+            mcs = early.tile([P, size, H], F32, name="mcs")
             engine.tensor_tensor(out=mcs[:], in0=mc[:, :, 0, :], in1=mc[:, :, 1, :], op=ALU.add)
-            return mcs
+            gh_so = early.tile([P, size, H], F32, name="gh_so")
+            engine.tensor_tensor(
+                out=gh_so[:],
+                in0=inputs[j]["grad"][:, :, 0:H],
+                in1=functions[j]["sig"][:, :, H : 2 * H],
+                op=ALU.mult,
+            )
+            return {"mcs": mcs, "gh_so": gh_so}
 
         def gate_gradients(j):
-            n = CHUNK_SIZES[j]
+            size = CHUNK_SIZES[j]
             x = inputs[j]
-            a = functions[j]
-            gh = x["g"][:, :, 0:H]
-            gc = x["g"][:, :, H : 2 * H]
-            s_i = a["sig"][:, :, 0:H]
-            s_o = a["sig"][:, :, H : 2 * H]
-            t_u = a["th"][:, 0]
-            t_c = a["th"][:, 1]
-            t_u2 = a["th2"][:, 0]
-            t_c2 = a["th2"][:, 1]
+            fn = functions[j]
+            mcs = early_of[j]["mcs"]
+            gh_so = early_of[j]["gh_so"]
+            gc = x["grad"][:, :, H : 2 * H]
+            s_i = fn["sig"][:, :, 0:H]
+            s_o = fn["sig"][:, :, H : 2 * H]
+            t_u = fn["th"][:, 0]
+            t_c = fn["th"][:, 1]
+            t_u2 = fn["th2"][:, 0]
+            t_c2 = fn["th2"][:, 1]
 
-            dz = mx.tile([P, n, K], BF16, name="dz")
-            q = work.tile([P, n, H], F32, name="q")
-            nc.vector.tensor_tensor(out=q[:], in0=gh, in1=s_o, op=ALU.mult)
-            e_o = work.tile([P, n, H], F32, name="e_o")
+            dz = mx.tile([P, size, K], BF16, name="dz")
+            e_o = work.tile([P, size, H], F32, name="e_o")
             nc.vector.scalar_tensor_tensor(
                 out=e_o[:], in0=s_o, scalar=1.0, in1=t_c, op0=ALU.subtract, op1=ALU.mult
             )
-            e_i = work.tile([P, n, H], F32, name="e_i")
+            e_i = work.tile([P, size, H], F32, name="e_i")
             nc.vector.scalar_tensor_tensor(
                 out=e_i[:], in0=s_i, scalar=1.0, in1=t_u, op0=ALU.subtract, op1=ALU.mult
             )
-            r = work.tile([P, n, H], F32, name="r")
+            x_neg = work.tile([P, size, H], F32, name="x_neg")
             nc.vector.scalar_tensor_tensor(
-                out=r[:], in0=t_c2, scalar=1.0, in1=q[:], op0=ALU.subtract, op1=ALU.mult
+                out=x_neg[:], in0=t_c2, scalar=1.0, in1=gh_so[:], op0=ALU.subtract, op1=ALU.mult
             )
-            if j < FIRST_GPSIMD_CHUNK:
-                mcs_of[j] = children_sum(nc.vector, j)
             nc.vector.scalar_tensor_tensor(
-                out=dz[:, :, H : 2 * H], in0=e_o[:], scalar=-1.0, in1=q[:], op0=ALU.mult, op1=ALU.mult
+                out=dz[:, :, H : 2 * H],
+                in0=e_o[:],
+                scalar=-1.0,
+                in1=gh_so[:],
+                op0=ALU.mult,
+                op1=ALU.mult,
             )
-            dc_neg = work.tile([P, n, H], F32, name="dc_neg")
-            nc.vector.tensor_tensor(out=dc_neg[:], in0=r[:], in1=gc, op=ALU.subtract)
-            diff = signs.tile([P, n, H], BF16, name="diff")
+            dc_neg = work.tile([P, size, H], F32, name="dc_neg")
+            nc.vector.tensor_tensor(out=dc_neg[:], in0=x_neg[:], in1=gc, op=ALU.subtract)
+            diff = signs.tile([P, size, H], BF16, name="diff")
             nc.vector.tensor_tensor(
                 out=diff[:], in0=x["mh"][:, :, 0, :], in1=x["mh"][:, :, 1, :], op=ALU.subtract
             )
-            p = work.tile([P, n, H], F32, name="p")
-            nc.vector.tensor_tensor(out=p[:], in0=dc_neg[:], in1=s_i, op=ALU.mult)
-            g_f = work.tile([P, n, H], F32, name="g_f")
+            dc_si_neg = work.tile([P, size, H], F32, name="dc_si_neg")
+            nc.vector.tensor_tensor(out=dc_si_neg[:], in0=dc_neg[:], in1=s_i, op=ALU.mult)
+            f_term = work.tile([P, size, H], F32, name="f_term")
             nc.vector.scalar_tensor_tensor(
-                out=g_f[:], in0=a["fc2"][:], scalar=0.25, in1=mcs_of[j][:], op0=ALU.subtract, op1=ALU.mult
-            )
-            nc.vector.tensor_tensor(out=dz[:, :, 0:H], in0=e_i[:], in1=p[:], op=ALU.mult)
-            nc.vector.scalar_tensor_tensor(
-                out=dz[:, :, 2 * H : 3 * H], in0=t_u2, scalar=1.0, in1=p[:], op0=ALU.subtract, op1=ALU.mult
+                out=f_term[:], in0=fn["fc2"][:], scalar=0.25, in1=mcs[:], op0=ALU.subtract, op1=ALU.mult
             )
             nc.vector.tensor_tensor(
-                out=dz[:, :, 3 * H : 4 * H], in0=g_f[:], in1=dc_neg[:], op=ALU.mult
+                out=dz[:, :, 0:H], in0=e_i[:], in1=dc_si_neg[:], op=ALU.mult
+            )
+            nc.vector.scalar_tensor_tensor(
+                out=dz[:, :, 2 * H : 3 * H],
+                in0=t_u2,
+                scalar=1.0,
+                in1=dc_si_neg[:],
+                op0=ALU.subtract,
+                op1=ALU.mult,
+            )
+            nc.vector.tensor_tensor(
+                out=dz[:, :, 3 * H : 4 * H], in0=f_term[:], in1=dc_neg[:], op=ALU.mult
             )
             return {"dz": dz, "diff": diff}
 
@@ -191,25 +212,25 @@ def tile_treelstmcellv2_t_v_kernel(
             return sgn
 
         def transpose_dz(j):
-            n = CHUNK_SIZES[j]
+            size = CHUNK_SIZES[j]
             dz = gradients[j]["dz"]
-            grouped = mx.tile([P, n * K], BF16, name="grouped", align_bytes=64)
-            for t in range(n):
+            grouped = mx.tile([P, size * K], BF16, name="grouped", align_bytes=64)
+            for t in range(size):
                 dz_t = psum_t.tile([P, K_BLOCKS, P], BF16, name="dz_t")
-                for b in range(K_BLOCKS):
-                    nc.tensor.transpose(dz_t[:, b, :], dz[:, t, b * P : (b + 1) * P], ident[:])
+                for blk in range(K_BLOCKS):
+                    nc.tensor.transpose(dz_t[:, blk, :], dz[:, t, blk * P : (blk + 1) * P], ident[:])
                 nc.scalar.copy(
                     out=grouped[:, t * K : (t + 1) * K].rearrange(
-                        "p (g r u) -> p g r u", g=PASSES, u=PACK
+                        "p (g node v) -> p g node v", g=PASSES, v=PACK
                     ),
-                    in_=dz_t[:].rearrange("p (g u) r -> p g r u", u=PACK),
+                    in_=dz_t[:].rearrange("p (g v) node -> p g node v", v=PACK),
                 )
             return grouped
 
         def quantise(j):
-            n = CHUNK_SIZES[j]
-            codes = mx.tile([P, n * PASSES * P], U32, name="codes", align_bytes=64)
-            scales = mx.tile([P, n * PASSES * P], U8, name="scales", align_bytes=64)
+            size = CHUNK_SIZES[j]
+            codes = mx.tile([P, size * PASSES * P], U32, name="codes", align_bytes=64)
+            scales = mx.tile([P, size * PASSES * P], U8, name="scales", align_bytes=64)
             nc.vector.quantize_mx(
                 out=codes[:].bitcast(E5M2X4), scales=scales[:], in_=grouped_dz[j][:]
             )
@@ -275,7 +296,7 @@ def tile_treelstmcellv2_t_v_kernel(
             nc.sync.dma_start(out=out_v[:, first_group[j] + t], in_=o_sb[:])
 
         functions = {}
-        mcs_of = {}
+        early_of = {}
         gradients = {}
         sign_of = {}
         grouped_dz = {}
@@ -287,13 +308,15 @@ def tile_treelstmcellv2_t_v_kernel(
             if j + 1 < CHUNKS:
                 functions[j + 1] = activations(j + 1)
             if j < CHUNKS:
+                if j < FIRST_GPSIMD_CHUNK:
+                    early_of[j] = early_results(nc.vector, j)
                 gradients[j] = gate_gradients(j)
                 sign_of[j] = child_sign(j)
                 grouped_dz[j] = transpose_dz(j)
             if j + LOADS_AHEAD < CHUNKS:
                 inputs[j + LOADS_AHEAD] = load(j + LOADS_AHEAD)
             if FIRST_GPSIMD_CHUNK <= j + 1 < CHUNKS:
-                mcs_of[j + 1] = children_sum(nc.gpsimd, j + 1)
+                early_of[j + 1] = early_results(nc.gpsimd, j + 1)
             if 1 <= j <= CHUNKS:
                 quantised[j - 1] = quantise(j - 1)
             if j >= 2:

@@ -27,7 +27,11 @@ GROUPS_PER_CHUNK = 2
 CHUNK_SIZES = [GROUPS_PER_CHUNK] * (GROUPS // GROUPS_PER_CHUNK - 1) + [1] * GROUPS_PER_CHUNK
 CHUNKS = len(CHUNK_SIZES)
 LOADS_AHEAD = 3
-FIRST_GPSIMD_CHUNK = 3
+FIRST_GPSIMD_CHUNK = 2
+PE_SUM_CHUNKS = 6
+VECTOR_SUM_CHUNKS = (6,)
+BLOCKS_EARLY = (0, 1, 4, 5, 6, 7)
+BLOCKS_LATE = (2, 3)
 
 FLOPS = 2 * NODES * K * N_OUT
 
@@ -54,11 +58,12 @@ def tile_treelstmcellv2_t_v_kernel(
         work = ctx.enter_context(tc.tile_pool(name="work", bufs=2))
         mx = ctx.enter_context(tc.tile_pool(name="mx", bufs=2))
         results = ctx.enter_context(tc.tile_pool(name="results", bufs=2))
-        signs = ctx.enter_context(tc.tile_pool(name="signs", bufs=3))
+        signs = ctx.enter_context(tc.tile_pool(name="signs", bufs=2))
         early = ctx.enter_context(tc.tile_pool(name="early", bufs=1))
         stores = ctx.enter_context(tc.tile_pool(name="stores", bufs=4))
         psum_t = ctx.enter_context(tc.psum_pool(name="psum_t", bufs=2))
-        psum_o = ctx.enter_context(tc.psum_pool(name="psum_o", bufs=3))
+        psum_m = ctx.enter_context(tc.psum_pool(name="psum_m", bufs=2))
+        psum_o = ctx.enter_context(tc.psum_pool(name="psum_o", bufs=2))
 
         w_rows = const.tile([P, K_BLOCKS, N_OUT], BF16, name="w_rows")
         iou_w_v = U_iou_w.rearrange("(blk p) n -> p blk n", p=P)
@@ -122,18 +127,33 @@ def tile_treelstmcellv2_t_v_kernel(
             nc.scalar.activation(out=sig[:], in_=x["iou"][:, :, 0 : 2 * H], func=ACT.Sigmoid)
             th = acts.tile([P, 2, size, H], F32, name="th")
             nc.scalar.activation(out=th[:, 1], in_=x["c"][:], func=ACT.Tanh)
+            not_o = acts.tile([P, size, H], F32, name="not_o")
+            nc.scalar.activation(
+                out=not_o[:], in_=x["iou"][:, :, H : 2 * H], func=ACT.Sigmoid, scale=-1.0
+            )
+            fc2 = acts.tile([P, size, H], F32, name="fc2")
+            nc.scalar.activation(out=fc2[:], in_=x["f"][:], func=ACT.Square, bias=neg_half[:, 0:1])
             nc.scalar.activation(out=th[:, 0], in_=x["iou"][:, :, 2 * H : 3 * H], func=ACT.Tanh)
             th2 = acts.tile([P, 2, size, H], F32, name="th2")
             nc.scalar.activation(out=th2[:], in_=th[:], func=ACT.Square)
-            fc2 = acts.tile([P, size, H], F32, name="fc2")
-            nc.scalar.activation(out=fc2[:], in_=x["f"][:], func=ACT.Square, bias=neg_half[:, 0:1])
-            return {"sig": sig, "th": th, "th2": th2, "fc2": fc2}
+            return {"sig": sig, "th": th, "th2": th2, "fc2": fc2, "not_o": not_o}
+
+        def children_sum_pe(j):
+            mc = inputs[j]["mc"]
+            mcs = psum_m.tile([P, CHUNK_SIZES[j], H], F32, name="mcs_ps")
+            for t in range(CHUNK_SIZES[j]):
+                nc.tensor.matmul(out=mcs[:, t, :], lhsT=ident[:], rhs=mc[:, t, 0, :], start=True, stop=False)
+                nc.tensor.matmul(out=mcs[:, t, :], lhsT=ident[:], rhs=mc[:, t, 1, :], start=False, stop=True)
+            return mcs
+
+        def children_sum(engine, j):
+            mc = inputs[j]["mc"]
+            mcs = early.tile([P, CHUNK_SIZES[j], H], F32, name="mcs")
+            engine.tensor_tensor(out=mcs[:], in0=mc[:, :, 0, :], in1=mc[:, :, 1, :], op=ALU.add)
+            return mcs
 
         def early_results(engine, j):
             size = CHUNK_SIZES[j]
-            mc = inputs[j]["mc"]
-            mcs = early.tile([P, size, H], F32, name="mcs")
-            engine.tensor_tensor(out=mcs[:], in0=mc[:, :, 0, :], in1=mc[:, :, 1, :], op=ALU.add)
             gh_so = early.tile([P, size, H], F32, name="gh_so")
             engine.tensor_tensor(
                 out=gh_so[:],
@@ -141,68 +161,79 @@ def tile_treelstmcellv2_t_v_kernel(
                 in1=functions[j]["sig"][:, :, H : 2 * H],
                 op=ALU.mult,
             )
-            return {"mcs": mcs, "gh_so": gh_so}
+            e_o = early.tile([P, size, H], F32, name="e_o")
+            engine.tensor_tensor(
+                out=e_o[:], in0=functions[j]["not_o"][:], in1=functions[j]["th"][:, 1], op=ALU.mult
+            )
+            return {"gh_so": gh_so, "e_o": e_o}
 
-        def gate_gradients(j):
-            size = CHUNK_SIZES[j]
-            x = inputs[j]
-            fn = functions[j]
-            mcs = early_of[j]["mcs"]
-            gh_so = early_of[j]["gh_so"]
-            gc = x["grad"][:, :, H : 2 * H]
-            s_i = fn["sig"][:, :, 0:H]
-            s_o = fn["sig"][:, :, H : 2 * H]
-            t_u = fn["th"][:, 0]
-            t_c = fn["th"][:, 1]
-            t_u2 = fn["th2"][:, 0]
-            t_c2 = fn["th2"][:, 1]
-
-            dz = mx.tile([P, size, K], BF16, name="dz")
-            e_o = work.tile([P, size, H], F32, name="e_o")
+        def forget_term(j):
+            f_term = work.tile([P, CHUNK_SIZES[j], H], F32, name="f_term")
             nc.vector.scalar_tensor_tensor(
-                out=e_o[:], in0=s_o, scalar=1.0, in1=t_c, op0=ALU.subtract, op1=ALU.mult
+                out=f_term[:],
+                in0=functions[j]["fc2"][:],
+                scalar=0.25,
+                in1=sum_of[j][:],
+                op0=ALU.subtract,
+                op1=ALU.mult,
+            )
+            return f_term
+
+        def gradients_first(j):
+            size = CHUNK_SIZES[j]
+            fn = functions[j]
+            x_neg = work.tile([P, size, H], F32, name="x_neg")
+            nc.vector.scalar_tensor_tensor(
+                out=x_neg[:],
+                in0=fn["th2"][:, 1],
+                scalar=1.0,
+                in1=early_of[j]["gh_so"][:],
+                op0=ALU.subtract,
+                op1=ALU.mult,
             )
             e_i = work.tile([P, size, H], F32, name="e_i")
             nc.vector.scalar_tensor_tensor(
-                out=e_i[:], in0=s_i, scalar=1.0, in1=t_u, op0=ALU.subtract, op1=ALU.mult
-            )
-            x_neg = work.tile([P, size, H], F32, name="x_neg")
-            nc.vector.scalar_tensor_tensor(
-                out=x_neg[:], in0=t_c2, scalar=1.0, in1=gh_so[:], op0=ALU.subtract, op1=ALU.mult
-            )
-            nc.vector.scalar_tensor_tensor(
-                out=dz[:, :, H : 2 * H],
-                in0=e_o[:],
-                scalar=-1.0,
-                in1=gh_so[:],
-                op0=ALU.mult,
+                out=e_i[:],
+                in0=fn["sig"][:, :, 0:H],
+                scalar=1.0,
+                in1=fn["th"][:, 0],
+                op0=ALU.subtract,
                 op1=ALU.mult,
             )
+            return {"x_neg": x_neg, "e_i": e_i}
+
+        def gradients_rest(j):
+            size = CHUNK_SIZES[j]
+            x = inputs[j]
+            fn = functions[j]
+            s_i = fn["sig"][:, :, 0:H]
+            dz = mx.tile([P, size, K], BF16, name="dz")
             dc_neg = work.tile([P, size, H], F32, name="dc_neg")
-            nc.vector.tensor_tensor(out=dc_neg[:], in0=x_neg[:], in1=gc, op=ALU.subtract)
+            nc.vector.tensor_tensor(
+                out=dc_neg[:], in0=first_of[j]["x_neg"][:], in1=x["grad"][:, :, H : 2 * H], op=ALU.subtract
+            )
             diff = signs.tile([P, size, H], BF16, name="diff")
             nc.vector.tensor_tensor(
                 out=diff[:], in0=x["mh"][:, :, 0, :], in1=x["mh"][:, :, 1, :], op=ALU.subtract
             )
             dc_si_neg = work.tile([P, size, H], F32, name="dc_si_neg")
             nc.vector.tensor_tensor(out=dc_si_neg[:], in0=dc_neg[:], in1=s_i, op=ALU.mult)
-            f_term = work.tile([P, size, H], F32, name="f_term")
-            nc.vector.scalar_tensor_tensor(
-                out=f_term[:], in0=fn["fc2"][:], scalar=0.25, in1=mcs[:], op0=ALU.subtract, op1=ALU.mult
+            nc.vector.tensor_tensor(
+                out=dz[:, :, 3 * H : 4 * H], in0=term_of[j][:], in1=dc_neg[:], op=ALU.mult
             )
             nc.vector.tensor_tensor(
-                out=dz[:, :, 0:H], in0=e_i[:], in1=dc_si_neg[:], op=ALU.mult
+                out=dz[:, :, 0:H], in0=first_of[j]["e_i"][:], in1=dc_si_neg[:], op=ALU.mult
             )
             nc.vector.scalar_tensor_tensor(
                 out=dz[:, :, 2 * H : 3 * H],
-                in0=t_u2,
+                in0=fn["th2"][:, 0],
                 scalar=1.0,
                 in1=dc_si_neg[:],
                 op0=ALU.subtract,
                 op1=ALU.mult,
             )
             nc.vector.tensor_tensor(
-                out=dz[:, :, 3 * H : 4 * H], in0=f_term[:], in1=dc_neg[:], op=ALU.mult
+                out=dz[:, :, H : 2 * H], in0=early_of[j]["e_o"][:], in1=early_of[j]["gh_so"][:], op=ALU.mult
             )
             return {"dz": dz, "diff": diff}
 
@@ -215,15 +246,20 @@ def tile_treelstmcellv2_t_v_kernel(
             size = CHUNK_SIZES[j]
             dz = gradients[j]["dz"]
             grouped = mx.tile([P, size * K], BF16, name="grouped", align_bytes=64)
+            banks = []
             for t in range(size):
                 dz_t = psum_t.tile([P, K_BLOCKS, P], BF16, name="dz_t")
-                for blk in range(K_BLOCKS):
+                banks.append(dz_t)
+                for blk in BLOCKS_EARLY:
                     nc.tensor.transpose(dz_t[:, blk, :], dz[:, t, blk * P : (blk + 1) * P], ident[:])
+            for t in range(size):
+                for blk in BLOCKS_LATE:
+                    nc.tensor.transpose(banks[t][:, blk, :], dz[:, t, blk * P : (blk + 1) * P], ident[:])
                 nc.scalar.copy(
                     out=grouped[:, t * K : (t + 1) * K].rearrange(
                         "p (g node v) -> p g node v", g=PASSES, v=PACK
                     ),
-                    in_=dz_t[:].rearrange("p (g v) node -> p g node v", v=PACK),
+                    in_=banks[t][:].rearrange("p (g v) node -> p g node v", v=PACK),
                 )
             return grouped
 
@@ -296,33 +332,46 @@ def tile_treelstmcellv2_t_v_kernel(
             nc.sync.dma_start(out=out_v[:, first_group[j] + t], in_=o_sb[:])
 
         functions = {}
+        sum_of = {}
         early_of = {}
+        term_of = {}
+        first_of = {}
         gradients = {}
         sign_of = {}
         grouped_dz = {}
         quantised = {}
         products = {}
         part_of = {}
-        functions[0] = activations(0)
-        for j in range(CHUNKS + 2):
-            if j + 1 < CHUNKS:
-                functions[j + 1] = activations(j + 1)
-            if j < CHUNKS:
-                if j < FIRST_GPSIMD_CHUNK:
-                    early_of[j] = early_results(nc.vector, j)
-                gradients[j] = gate_gradients(j)
+        for j in range(-1, CHUNKS + 1):
+            nxt = j + 1
+            if nxt < CHUNKS:
+                functions[nxt] = activations(nxt)
+                if nxt < PE_SUM_CHUNKS:
+                    sum_of[nxt] = children_sum_pe(nxt)
+            if 0 <= j < CHUNKS:
+                first_of[j] = gradients_first(j)
+                if j >= PE_SUM_CHUNKS:
+                    if j in VECTOR_SUM_CHUNKS:
+                        sum_of[j] = children_sum(nc.vector, j)
+                    term_of[j] = forget_term(j)
+            if 1 <= j:
+                quantised[j - 1] = quantise(j - 1)
+                for t in range(CHUNK_SIZES[j - 1]):
+                    products[j - 1, t] = multiply(j - 1, t)
+            if 0 <= j < CHUNKS:
+                gradients[j] = gradients_rest(j)
                 sign_of[j] = child_sign(j)
                 grouped_dz[j] = transpose_dz(j)
-            if j + LOADS_AHEAD < CHUNKS:
+            if 0 <= j and j + LOADS_AHEAD < CHUNKS:
                 inputs[j + LOADS_AHEAD] = load(j + LOADS_AHEAD)
-            if FIRST_GPSIMD_CHUNK <= j + 1 < CHUNKS:
-                early_of[j + 1] = early_results(nc.gpsimd, j + 1)
-            if 1 <= j <= CHUNKS:
-                quantised[j - 1] = quantise(j - 1)
-            if j >= 2:
-                part_of[j - 2] = shared_part(j - 2)
-            for t in range(GROUPS_PER_CHUNK):
-                if 1 <= j <= CHUNKS and t < CHUNK_SIZES[j - 1]:
-                    products[j - 1, t] = multiply(j - 1, t)
-                if j >= 2 and t < CHUNK_SIZES[j - 2]:
-                    finish(j - 2, t)
+            if nxt < CHUNKS:
+                engine = nc.gpsimd if nxt >= FIRST_GPSIMD_CHUNK else nc.vector
+                early_of[nxt] = early_results(engine, nxt)
+                if nxt >= PE_SUM_CHUNKS and nxt not in VECTOR_SUM_CHUNKS:
+                    sum_of[nxt] = children_sum(nc.gpsimd, nxt)
+                if nxt < PE_SUM_CHUNKS:
+                    term_of[nxt] = forget_term(nxt)
+            if 1 <= j:
+                part_of[j - 1] = shared_part(j - 1)
+                for t in range(CHUNK_SIZES[j - 1]):
+                    finish(j - 1, t)

@@ -27,7 +27,7 @@ GROUPS_PER_CHUNK = 2
 CHUNK_SIZES = [GROUPS_PER_CHUNK] * (GROUPS // GROUPS_PER_CHUNK - 1) + [1] * GROUPS_PER_CHUNK
 CHUNKS = len(CHUNK_SIZES)
 LOADS_AHEAD = 3
-FIRST_GPSIMD_CHUNK = 2
+FIRST_GPSIMD_CHUNK = 3
 PE_SUM_CHUNKS = 6
 VECTOR_SUM_CHUNKS = (6,)
 BLOCKS_EARLY = (0, 1, 4, 5, 6, 7)
@@ -58,7 +58,7 @@ def tile_treelstmcellv2_t_v_kernel(
         work = ctx.enter_context(tc.tile_pool(name="work", bufs=2))
         mx = ctx.enter_context(tc.tile_pool(name="mx", bufs=2))
         results = ctx.enter_context(tc.tile_pool(name="results", bufs=2))
-        signs = ctx.enter_context(tc.tile_pool(name="signs", bufs=2))
+        signs = ctx.enter_context(tc.tile_pool(name="signs", bufs=3))
         early = ctx.enter_context(tc.tile_pool(name="early", bufs=1))
         stores = ctx.enter_context(tc.tile_pool(name="stores", bufs=4))
         psum_t = ctx.enter_context(tc.psum_pool(name="psum_t", bufs=2))
@@ -232,10 +232,15 @@ def tile_treelstmcellv2_t_v_kernel(
                 op0=ALU.subtract,
                 op1=ALU.mult,
             )
-            nc.vector.tensor_tensor(
-                out=dz[:, :, H : 2 * H], in0=early_of[j]["e_o"][:], in1=early_of[j]["gh_so"][:], op=ALU.mult
-            )
             return {"dz": dz, "diff": diff}
+
+        def output_gate(j):
+            nc.vector.tensor_tensor(
+                out=gradients[j]["dz"][:, :, H : 2 * H],
+                in0=early_of[j]["e_o"][:],
+                in1=early_of[j]["gh_so"][:],
+                op=ALU.mult,
+            )
 
         def child_sign(j):
             sgn = signs.tile([P, CHUNK_SIZES[j], H], BF16, name="sgn")
@@ -342,7 +347,7 @@ def tile_treelstmcellv2_t_v_kernel(
         quantised = {}
         products = {}
         part_of = {}
-        for j in range(-1, CHUNKS + 1):
+        for j in range(-1, CHUNKS + 2):
             nxt = j + 1
             if nxt < CHUNKS:
                 functions[nxt] = activations(nxt)
@@ -354,12 +359,11 @@ def tile_treelstmcellv2_t_v_kernel(
                     if j in VECTOR_SUM_CHUNKS:
                         sum_of[j] = children_sum(nc.vector, j)
                     term_of[j] = forget_term(j)
-            if 1 <= j:
-                quantised[j - 1] = quantise(j - 1)
-                for t in range(CHUNK_SIZES[j - 1]):
-                    products[j - 1, t] = multiply(j - 1, t)
-            if 0 <= j < CHUNKS:
                 gradients[j] = gradients_rest(j)
+            if 1 <= j <= CHUNKS:
+                quantised[j - 1] = quantise(j - 1)
+            if 0 <= j < CHUNKS:
+                output_gate(j)
                 sign_of[j] = child_sign(j)
                 grouped_dz[j] = transpose_dz(j)
             if 0 <= j and j + LOADS_AHEAD < CHUNKS:
@@ -371,7 +375,10 @@ def tile_treelstmcellv2_t_v_kernel(
                     sum_of[nxt] = children_sum(nc.gpsimd, nxt)
                 if nxt < PE_SUM_CHUNKS:
                     term_of[nxt] = forget_term(nxt)
-            if 1 <= j:
-                part_of[j - 1] = shared_part(j - 1)
-                for t in range(CHUNK_SIZES[j - 1]):
-                    finish(j - 1, t)
+            if j >= 2:
+                part_of[j - 2] = shared_part(j - 2)
+            for t in range(GROUPS_PER_CHUNK):
+                if j >= 2 and t < CHUNK_SIZES[j - 2]:
+                    finish(j - 2, t)
+                if 1 <= j <= CHUNKS and t < CHUNK_SIZES[j - 1]:
+                    products[j - 1, t] = multiply(j - 1, t)

@@ -127,16 +127,12 @@ def tile_treelstmcellv2_t_v_kernel(
             nc.scalar.activation(out=sig[:], in_=x["iou"][:, :, 0 : 2 * H], func=ACT.Sigmoid)
             th = acts.tile([P, 2, size, H], F32, name="th")
             nc.scalar.activation(out=th[:, 1], in_=x["c"][:], func=ACT.Tanh)
-            not_o = acts.tile([P, size, H], F32, name="not_o")
-            nc.scalar.activation(
-                out=not_o[:], in_=x["iou"][:, :, H : 2 * H], func=ACT.Sigmoid, scale=-1.0
-            )
             fc2 = acts.tile([P, size, H], F32, name="fc2")
             nc.scalar.activation(out=fc2[:], in_=x["f"][:], func=ACT.Square, bias=neg_half[:, 0:1])
             nc.scalar.activation(out=th[:, 0], in_=x["iou"][:, :, 2 * H : 3 * H], func=ACT.Tanh)
             th2 = acts.tile([P, 2, size, H], F32, name="th2")
             nc.scalar.activation(out=th2[:], in_=th[:], func=ACT.Square)
-            return {"sig": sig, "th": th, "th2": th2, "fc2": fc2, "not_o": not_o}
+            return {"sig": sig, "th": th, "th2": th2, "fc2": fc2}
 
         def children_sum_pe(j):
             mc = inputs[j]["mc"]
@@ -161,11 +157,7 @@ def tile_treelstmcellv2_t_v_kernel(
                 in1=functions[j]["sig"][:, :, H : 2 * H],
                 op=ALU.mult,
             )
-            e_o = early.tile([P, size, H], F32, name="e_o")
-            engine.tensor_tensor(
-                out=e_o[:], in0=functions[j]["not_o"][:], in1=functions[j]["th"][:, 1], op=ALU.mult
-            )
-            return {"gh_so": gh_so, "e_o": e_o}
+            return {"gh_so": gh_so}
 
         def forget_term(j):
             f_term = work.tile([P, CHUNK_SIZES[j], H], F32, name="f_term")
@@ -182,12 +174,12 @@ def tile_treelstmcellv2_t_v_kernel(
         def gradients_first(j):
             size = CHUNK_SIZES[j]
             fn = functions[j]
-            x_neg = work.tile([P, size, H], F32, name="x_neg")
+            e_o = work.tile([P, size, H], F32, name="e_o")
             nc.vector.scalar_tensor_tensor(
-                out=x_neg[:],
-                in0=fn["th2"][:, 1],
+                out=e_o[:],
+                in0=fn["sig"][:, :, H : 2 * H],
                 scalar=1.0,
-                in1=early_of[j]["gh_so"][:],
+                in1=fn["th"][:, 1],
                 op0=ALU.subtract,
                 op1=ALU.mult,
             )
@@ -200,7 +192,16 @@ def tile_treelstmcellv2_t_v_kernel(
                 op0=ALU.subtract,
                 op1=ALU.mult,
             )
-            return {"x_neg": x_neg, "e_i": e_i}
+            x_neg = work.tile([P, size, H], F32, name="x_neg")
+            nc.vector.scalar_tensor_tensor(
+                out=x_neg[:],
+                in0=fn["th2"][:, 1],
+                scalar=1.0,
+                in1=early_of[j]["gh_so"][:],
+                op0=ALU.subtract,
+                op1=ALU.mult,
+            )
+            return {"x_neg": x_neg, "e_i": e_i, "e_o": e_o}
 
         def gradients_rest(j):
             size = CHUNK_SIZES[j]
@@ -235,11 +236,13 @@ def tile_treelstmcellv2_t_v_kernel(
             return {"dz": dz, "diff": diff}
 
         def output_gate(j):
-            nc.vector.tensor_tensor(
+            nc.vector.scalar_tensor_tensor(
                 out=gradients[j]["dz"][:, :, H : 2 * H],
-                in0=early_of[j]["e_o"][:],
+                in0=first_of[j]["e_o"][:],
+                scalar=-1.0,
                 in1=early_of[j]["gh_so"][:],
-                op=ALU.mult,
+                op0=ALU.mult,
+                op1=ALU.mult,
             )
 
         def child_sign(j):
@@ -355,9 +358,9 @@ def tile_treelstmcellv2_t_v_kernel(
                     sum_of[nxt] = children_sum_pe(nxt)
             if 0 <= j < CHUNKS:
                 first_of[j] = gradients_first(j)
+                if j in VECTOR_SUM_CHUNKS:
+                    sum_of[j] = children_sum(nc.vector, j)
                 if j >= PE_SUM_CHUNKS:
-                    if j in VECTOR_SUM_CHUNKS:
-                        sum_of[j] = children_sum(nc.vector, j)
                     term_of[j] = forget_term(j)
                 gradients[j] = gradients_rest(j)
             if 1 <= j <= CHUNKS:

@@ -7,6 +7,7 @@ F32 = mybir.dt.float32
 BF16 = mybir.dt.bfloat16
 U32 = mybir.dt.uint32
 U8 = mybir.dt.uint8
+I32 = mybir.dt.int32
 E4M3X4 = mybir.dt.float8_e4m3fn_x4
 E5M2X4 = mybir.dt.float8_e5m2_x4
 ALU = mybir.AluOpType
@@ -28,10 +29,11 @@ CHUNK_SIZES = [GROUPS_PER_CHUNK] * (GROUPS // GROUPS_PER_CHUNK - 1) + [1] * GROU
 CHUNKS = len(CHUNK_SIZES)
 LOADS_AHEAD = 3
 FIRST_GPSIMD_CHUNK = 3
-PE_SUM_CHUNKS = 6
-VECTOR_SUM_CHUNKS = (6,)
+PE_SUM_CHUNKS = (1, 2, 3, 4, 5, 6)
+VECTOR_SUM_CHUNKS = (0,)
 BLOCKS_EARLY = (0, 1, 4, 5, 6, 7)
 BLOCKS_LATE = (2, 3)
+LEAN_CHUNKS = (7, 8)
 
 FLOPS = 2 * NODES * K * N_OUT
 
@@ -99,8 +101,10 @@ def tile_treelstmcellv2_t_v_kernel(
         nc.vector.memset(neg_half[:], -0.5)
 
         w_grouped = const.tile([P, PASSES, N_OUT, PACK], BF16, name="w_grouped", align_bytes=64)
-        w_codes = const.tile([P, PASSES, N_OUT + H], U32, name="w_codes", align_bytes=64)
-        w_scales = const.tile([P, PASSES, N_OUT + H], U8, name="w_scales", align_bytes=64)
+        w_codes = const.tile([P, PASSES * N_OUT + H], U32, name="w_codes", align_bytes=64)
+        w_scales = const.tile([P, PASSES * N_OUT + H], U8, name="w_scales", align_bytes=64)
+        nc.vector.memset(w_codes[:, PASSES * N_OUT :].bitcast(I32), 0)
+        nc.vector.memset(w_scales[:, PASSES * N_OUT :].bitcast(I32), 0)
         for g in range(PASSES):
             nc.vector.tensor_copy(
                 out=w_grouped[:, g].rearrange("p (run i) v -> p run v i", i=COPY_RUN),
@@ -110,14 +114,9 @@ def tile_treelstmcellv2_t_v_kernel(
             )
         for g in range(PASSES):
             nc.vector.quantize_mx(
-                out=w_codes[:, g, 0:N_OUT].bitcast(E4M3X4),
-                scales=w_scales[:, g, 0:N_OUT],
+                out=w_codes[:, g * N_OUT : (g + 1) * N_OUT].bitcast(E4M3X4),
+                scales=w_scales[:, g * N_OUT : (g + 1) * N_OUT],
                 in_=w_grouped[:, g].rearrange("p n v -> p (n v)"),
-            )
-            nc.vector.quantize_mx(
-                out=w_codes[:, g, N_OUT : N_OUT + H].bitcast(E4M3X4),
-                scales=w_scales[:, g, N_OUT : N_OUT + H],
-                in_=w_grouped[:, g, 0:H, :].rearrange("p n v -> p (n v)"),
             )
 
         def activations(j):
@@ -127,11 +126,12 @@ def tile_treelstmcellv2_t_v_kernel(
             nc.scalar.activation(out=sig[:], in_=x["iou"][:, :, 0 : 2 * H], func=ACT.Sigmoid)
             th = acts.tile([P, 2, size, H], F32, name="th")
             nc.scalar.activation(out=th[:, 1], in_=x["c"][:], func=ACT.Tanh)
+            th2 = acts.tile([P, 2, size, H], F32, name="th2")
+            nc.scalar.activation(out=th2[:, 1], in_=th[:, 1], func=ACT.Square)
+            nc.scalar.activation(out=th[:, 0], in_=x["iou"][:, :, 2 * H : 3 * H], func=ACT.Tanh)
+            nc.scalar.activation(out=th2[:, 0], in_=th[:, 0], func=ACT.Square)
             fc2 = acts.tile([P, size, H], F32, name="fc2")
             nc.scalar.activation(out=fc2[:], in_=x["f"][:], func=ACT.Square, bias=neg_half[:, 0:1])
-            nc.scalar.activation(out=th[:, 0], in_=x["iou"][:, :, 2 * H : 3 * H], func=ACT.Tanh)
-            th2 = acts.tile([P, 2, size, H], F32, name="th2")
-            nc.scalar.activation(out=th2[:], in_=th[:], func=ACT.Square)
             return {"sig": sig, "th": th, "th2": th2, "fc2": fc2}
 
         def children_sum_pe(j):
@@ -183,15 +183,6 @@ def tile_treelstmcellv2_t_v_kernel(
                 op0=ALU.subtract,
                 op1=ALU.mult,
             )
-            e_i = work.tile([P, size, H], F32, name="e_i")
-            nc.vector.scalar_tensor_tensor(
-                out=e_i[:],
-                in0=fn["sig"][:, :, 0:H],
-                scalar=1.0,
-                in1=fn["th"][:, 0],
-                op0=ALU.subtract,
-                op1=ALU.mult,
-            )
             x_neg = work.tile([P, size, H], F32, name="x_neg")
             nc.vector.scalar_tensor_tensor(
                 out=x_neg[:],
@@ -201,7 +192,7 @@ def tile_treelstmcellv2_t_v_kernel(
                 op0=ALU.subtract,
                 op1=ALU.mult,
             )
-            return {"x_neg": x_neg, "e_i": e_i, "e_o": e_o}
+            return {"x_neg": x_neg, "e_o": e_o}
 
         def gradients_rest(j):
             size = CHUNK_SIZES[j]
@@ -209,21 +200,32 @@ def tile_treelstmcellv2_t_v_kernel(
             fn = functions[j]
             s_i = fn["sig"][:, :, 0:H]
             dz = mx.tile([P, size, K], BF16, name="dz")
-            dc_neg = work.tile([P, size, H], F32, name="dc_neg")
-            nc.vector.tensor_tensor(
-                out=dc_neg[:], in0=first_of[j]["x_neg"][:], in1=x["grad"][:, :, H : 2 * H], op=ALU.subtract
-            )
             diff = signs.tile([P, size, H], BF16, name="diff")
             nc.vector.tensor_tensor(
                 out=diff[:], in0=x["mh"][:, :, 0, :], in1=x["mh"][:, :, 1, :], op=ALU.subtract
             )
+            dc_neg = work.tile([P, size, H], F32, name="dc_neg")
+            nc.vector.tensor_tensor(
+                out=dc_neg[:], in0=first_of[j]["x_neg"][:], in1=x["grad"][:, :, H : 2 * H], op=ALU.subtract
+            )
+            e_i = work.tile([P, size, H], F32, name="e_i")
+            nc.vector.scalar_tensor_tensor(
+                out=e_i[:],
+                in0=fn["sig"][:, :, 0:H],
+                scalar=1.0,
+                in1=fn["th"][:, 0],
+                op0=ALU.subtract,
+                op1=ALU.mult,
+            )
+            if j not in PE_SUM_CHUNKS:
+                term_of[j] = forget_term(j)
             dc_si_neg = work.tile([P, size, H], F32, name="dc_si_neg")
             nc.vector.tensor_tensor(out=dc_si_neg[:], in0=dc_neg[:], in1=s_i, op=ALU.mult)
             nc.vector.tensor_tensor(
                 out=dz[:, :, 3 * H : 4 * H], in0=term_of[j][:], in1=dc_neg[:], op=ALU.mult
             )
             nc.vector.tensor_tensor(
-                out=dz[:, :, 0:H], in0=first_of[j]["e_i"][:], in1=dc_si_neg[:], op=ALU.mult
+                out=dz[:, :, 0:H], in0=e_i[:], in1=dc_si_neg[:], op=ALU.mult
             )
             nc.vector.scalar_tensor_tensor(
                 out=dz[:, :, 2 * H : 3 * H],
@@ -284,7 +286,9 @@ def tile_treelstmcellv2_t_v_kernel(
             codes = quantised[j]["codes"]
             scales = quantised[j]["scales"]
             dhc = psum_o.tile([P, N_OUT], F32, name="dhc")
-            both = psum_o.tile([P, N_OUT], F32, name="both")
+            both = None
+            if j not in LEAN_CHUNKS:
+                both = psum_o.tile([P, N_OUT], F32, name="both")
 
             def one_pass(acc, g, w_from, start, stop):
                 nodes = slice((t * PASSES + g) * P, (t * PASSES + g + 1) * P)
@@ -292,8 +296,8 @@ def tile_treelstmcellv2_t_v_kernel(
                     out=acc[:],
                     lhsT=codes[:, nodes].bitcast(E5M2X4),
                     lhsT_scale=scales[:, nodes],
-                    rhs=w_codes[:, g, w_from : w_from + N_OUT].bitcast(E4M3X4),
-                    rhs_scale=w_scales[:, g, w_from : w_from + N_OUT],
+                    rhs=w_codes[:, g * N_OUT + w_from : (g + 1) * N_OUT + w_from].bitcast(E4M3X4),
+                    rhs_scale=w_scales[:, g * N_OUT + w_from : (g + 1) * N_OUT + w_from],
                     start=start,
                     stop=stop,
                 )
@@ -302,8 +306,9 @@ def tile_treelstmcellv2_t_v_kernel(
                 first = g == 0
                 last = g == PASSES - 1
                 one_pass(dhc, g, 0, first, last)
-                one_pass(both, g, 0, first, False)
-                one_pass(both, g, H, False, last)
+                if j not in LEAN_CHUNKS:
+                    one_pass(both, g, 0, first, False)
+                    one_pass(both, g, H, False, last)
             return {"dhc": dhc, "both": both}
 
         def shared_part(j):
@@ -319,6 +324,19 @@ def tile_treelstmcellv2_t_v_kernel(
                 )
             return part
 
+        def other_part(j):
+            other = results.tile([P, CHUNK_SIZES[j], H], F32, name="other")
+            for t in range(CHUNK_SIZES[j]):
+                nc.vector.scalar_tensor_tensor(
+                    out=other[:, t],
+                    in0=sign_of[j][:, t],
+                    scalar=1.0,
+                    in1=products[j, t]["dhc"][:, H : 2 * H],
+                    op0=ALU.subtract,
+                    op1=ALU.mult,
+                )
+            return other
+
         def finish(j, t):
             o_sb = stores.tile([P, 2, H], F32, name="o_sb")
             nc.vector.scalar_tensor_tensor(
@@ -329,11 +347,12 @@ def tile_treelstmcellv2_t_v_kernel(
                 op0=ALU.mult,
                 op1=ALU.add,
             )
+            lean = j in LEAN_CHUNKS
             nc.vector.scalar_tensor_tensor(
                 out=o_sb[:, 1, :],
-                in0=part_of[j][:, t],
+                in0=(other_of[j] if lean else part_of[j])[:, t],
                 scalar=-0.5,
-                in1=products[j, t]["both"][:, 0:H],
+                in1=products[j, t]["dhc" if lean else "both"][:, 0:H],
                 op0=ALU.mult,
                 op1=ALU.add,
             )
@@ -350,18 +369,17 @@ def tile_treelstmcellv2_t_v_kernel(
         quantised = {}
         products = {}
         part_of = {}
+        other_of = {}
         for j in range(-1, CHUNKS + 2):
             nxt = j + 1
             if nxt < CHUNKS:
                 functions[nxt] = activations(nxt)
-                if nxt < PE_SUM_CHUNKS:
+                if nxt in PE_SUM_CHUNKS:
                     sum_of[nxt] = children_sum_pe(nxt)
             if 0 <= j < CHUNKS:
-                first_of[j] = gradients_first(j)
                 if j in VECTOR_SUM_CHUNKS:
                     sum_of[j] = children_sum(nc.vector, j)
-                if j >= PE_SUM_CHUNKS:
-                    term_of[j] = forget_term(j)
+                first_of[j] = gradients_first(j)
                 gradients[j] = gradients_rest(j)
             if 1 <= j <= CHUNKS:
                 quantised[j - 1] = quantise(j - 1)
@@ -374,14 +392,16 @@ def tile_treelstmcellv2_t_v_kernel(
             if nxt < CHUNKS:
                 engine = nc.gpsimd if nxt >= FIRST_GPSIMD_CHUNK else nc.vector
                 early_of[nxt] = early_results(engine, nxt)
-                if nxt >= PE_SUM_CHUNKS and nxt not in VECTOR_SUM_CHUNKS:
+                if nxt not in PE_SUM_CHUNKS and nxt not in VECTOR_SUM_CHUNKS:
                     sum_of[nxt] = children_sum(nc.gpsimd, nxt)
-                if nxt < PE_SUM_CHUNKS:
-                    term_of[nxt] = forget_term(nxt)
             if j >= 2:
                 part_of[j - 2] = shared_part(j - 2)
+                if j - 2 in LEAN_CHUNKS:
+                    other_of[j - 2] = other_part(j - 2)
             for t in range(GROUPS_PER_CHUNK):
                 if j >= 2 and t < CHUNK_SIZES[j - 2]:
                     finish(j - 2, t)
                 if 1 <= j <= CHUNKS and t < CHUNK_SIZES[j - 1]:
                     products[j - 1, t] = multiply(j - 1, t)
+            if nxt in PE_SUM_CHUNKS:
+                term_of[nxt] = forget_term(nxt)

@@ -15,6 +15,8 @@ ACT = mybir.ActivationFunctionType
 
 P = 128
 PACK = 4
+PAIR = 2
+GATES = 4
 NODES = 2048
 H = 256
 K = 4 * H
@@ -31,8 +33,8 @@ LOADS_AHEAD = 3
 FIRST_GPSIMD_CHUNK = 3
 PE_SUM_CHUNKS = (1, 2, 3, 4, 5, 6)
 VECTOR_SUM_CHUNKS = (0,)
-BLOCKS_EARLY = (0, 1, 4, 5, 6, 7)
-BLOCKS_LATE = (2, 3)
+GATES_EARLY = (0, 2, 3)
+GATES_LATE = (1,)
 LEAN_CHUNKS = (7, 8)
 
 FLOPS = 2 * NODES * K * N_OUT
@@ -68,11 +70,12 @@ def tile_treelstmcellv2_t_v_kernel(
         psum_o = ctx.enter_context(tc.psum_pool(name="psum_o", bufs=2))
 
         w_rows = const.tile([P, K_BLOCKS, N_OUT], BF16, name="w_rows")
-        iou_w_v = U_iou_w.rearrange("(blk p) n -> p blk n", p=P)
-        f_w_v = U_f_w.rearrange("(blk p) n -> p blk n", p=P)
-        nc.sync.dma_start(out=w_rows[:, 0:PACK, :], in_=iou_w_v[:, 0:PACK, :])
-        nc.sync.dma_start(out=w_rows[:, PACK:IOU_BLOCKS, :], in_=iou_w_v[:, PACK:IOU_BLOCKS, :])
-        nc.sync.dma_start(out=w_rows[:, IOU_BLOCKS:K_BLOCKS, :], in_=f_w_v)
+        w_pairs = w_rows[:].rearrange("p (b e) n -> p b (e n)", e=PAIR)
+        iou_w_v = U_iou_w.rearrange("(b p e) n -> p b (e n)", p=P, e=PAIR)
+        f_w_v = U_f_w.rearrange("(b p e) n -> p b (e n)", p=P, e=PAIR)
+        nc.sync.dma_start(out=w_pairs[:, 0:2, :], in_=iou_w_v[:, 0:2, :])
+        nc.sync.dma_start(out=w_pairs[:, 2:3, :], in_=iou_w_v[:, 2:3, :])
+        nc.sync.dma_start(out=w_pairs[:, 3:4, :], in_=f_w_v)
 
         def load(j):
             size = CHUNK_SIZES[j]
@@ -97,6 +100,8 @@ def tile_treelstmcellv2_t_v_kernel(
 
         ident = const.tile([P, P], BF16, name="ident")
         make_identity(nc, ident[:])
+        ident_f = const.tile([P, P], F32, name="ident_f")
+        make_identity(nc, ident_f[:])
         neg_half = const.tile([P, 1], F32, name="neg_half")
         nc.vector.memset(neg_half[:], -0.5)
 
@@ -258,18 +263,20 @@ def tile_treelstmcellv2_t_v_kernel(
             grouped = mx.tile([P, size * K], BF16, name="grouped", align_bytes=64)
             banks = []
             for t in range(size):
-                dz_t = psum_t.tile([P, K_BLOCKS, P], BF16, name="dz_t")
+                words = dz[:, t, :].bitcast(F32)
+                dz_t = psum_t.tile([P, GATES, P], F32, name="dz_t")
                 banks.append(dz_t)
-                for blk in BLOCKS_EARLY:
-                    nc.tensor.transpose(dz_t[:, blk, :], dz[:, t, blk * P : (blk + 1) * P], ident[:])
+                for b in GATES_EARLY:
+                    nc.tensor.transpose(dz_t[:, b, :], words[:, b * P : (b + 1) * P], ident_f[:])
             for t in range(size):
-                for blk in BLOCKS_LATE:
-                    nc.tensor.transpose(banks[t][:, blk, :], dz[:, t, blk * P : (blk + 1) * P], ident[:])
+                words = dz[:, t, :].bitcast(F32)
+                for b in GATES_LATE:
+                    nc.tensor.transpose(banks[t][:, b, :], words[:, b * P : (b + 1) * P], ident_f[:])
                 nc.scalar.copy(
-                    out=grouped[:, t * K : (t + 1) * K].rearrange(
-                        "p (g node v) -> p g node v", g=PASSES, v=PACK
-                    ),
-                    in_=banks[t][:].rearrange("p (g v) node -> p g node v", v=PACK),
+                    out=grouped[:, t * K : (t + 1) * K]
+                    .bitcast(F32)
+                    .rearrange("p (g node u) -> p g node u", g=PASSES, u=PAIR),
+                    in_=banks[t][:].rearrange("p (g u) node -> p g node u", u=PAIR),
                 )
             return grouped
 

@@ -23,6 +23,7 @@ K = 4 * H
 N_OUT = 2 * H
 PASSES = K // (P * PACK)
 K_BLOCKS = K // P
+H_BLOCKS = H // P
 IOU_BLOCKS = 3 * H // P
 COPY_RUN = 4
 GROUPS = NODES // P
@@ -32,7 +33,7 @@ CHUNKS = len(CHUNK_SIZES)
 LOADS_AHEAD = 3
 FIRST_GPSIMD_CHUNK = 3
 PE_SUM_CHUNKS = (1, 2, 3, 4, 5, 6)
-VECTOR_SUM_CHUNKS = (0,)
+VECTOR_SUM_CHUNKS = (0, 7, 8)
 GATES_EARLY = (0, 2, 3)
 GATES_LATE = (1,)
 LEAN_CHUNKS = (7, 8)
@@ -66,8 +67,9 @@ def tile_treelstmcellv2_t_v_kernel(
         early = ctx.enter_context(tc.tile_pool(name="early", bufs=1))
         stores = ctx.enter_context(tc.tile_pool(name="stores", bufs=4))
         psum_t = ctx.enter_context(tc.psum_pool(name="psum_t", bufs=2))
-        psum_m = ctx.enter_context(tc.psum_pool(name="psum_m", bufs=2))
-        psum_o = ctx.enter_context(tc.psum_pool(name="psum_o", bufs=2))
+        psum_m = ctx.enter_context(tc.psum_pool(name="psum_m", bufs=1))
+        psum_u = ctx.enter_context(tc.psum_pool(name="psum_u", bufs=1))
+        psum_o = ctx.enter_context(tc.psum_pool(name="psum_o", bufs=3))
 
         w_rows = const.tile([P, K_BLOCKS, N_OUT], BF16, name="w_rows")
         w_pairs = w_rows[:].rearrange("p (b e) n -> p b (e n)", e=PAIR)
@@ -106,10 +108,11 @@ def tile_treelstmcellv2_t_v_kernel(
         nc.vector.memset(neg_half[:], -0.5)
 
         w_grouped = const.tile([P, PASSES, N_OUT, PACK], BF16, name="w_grouped", align_bytes=64)
-        w_codes = const.tile([P, PASSES * N_OUT + H], U32, name="w_codes", align_bytes=64)
-        w_scales = const.tile([P, PASSES * N_OUT + H], U8, name="w_scales", align_bytes=64)
-        nc.vector.memset(w_codes[:, PASSES * N_OUT :].bitcast(I32), 0)
-        nc.vector.memset(w_scales[:, PASSES * N_OUT :].bitcast(I32), 0)
+        w_codes = const.tile([P, PASSES, N_OUT + H], U32, name="w_codes", align_bytes=64)
+        w_scales = const.tile([P, PASSES, N_OUT + H], U8, name="w_scales", align_bytes=64)
+        for g in range(PASSES):
+            nc.vector.memset(w_codes[:, g, N_OUT:].bitcast(I32), 0)
+            nc.vector.memset(w_scales[:, g, N_OUT:].bitcast(I32), 0)
         for g in range(PASSES):
             nc.vector.tensor_copy(
                 out=w_grouped[:, g].rearrange("p (run i) v -> p run v i", i=COPY_RUN),
@@ -119,25 +122,42 @@ def tile_treelstmcellv2_t_v_kernel(
             )
         for g in range(PASSES):
             nc.vector.quantize_mx(
-                out=w_codes[:, g * N_OUT : (g + 1) * N_OUT].bitcast(E4M3X4),
-                scales=w_scales[:, g * N_OUT : (g + 1) * N_OUT],
+                out=w_codes[:, g, 0:N_OUT].bitcast(E4M3X4),
+                scales=w_scales[:, g, 0:N_OUT],
                 in_=w_grouped[:, g].rearrange("p n v -> p (n v)"),
             )
 
         def activations(j):
             size = CHUNK_SIZES[j]
             x = inputs[j]
+            u_t = psum_u.tile([P, size, H], F32, name="u_t")
+            for t in range(size):
+                for blk in range(H_BLOCKS):
+                    cols = slice(blk * P, (blk + 1) * P)
+                    nc.tensor.transpose(
+                        u_t[:, t, cols], x["iou"][:, t, 2 * H + blk * P : 2 * H + (blk + 1) * P], ident_f[:]
+                    )
             sig = acts.tile([P, size, 2 * H], F32, name="sig")
             nc.scalar.activation(out=sig[:], in_=x["iou"][:, :, 0 : 2 * H], func=ACT.Sigmoid)
-            th = acts.tile([P, 2, size, H], F32, name="th")
-            nc.scalar.activation(out=th[:, 1], in_=x["c"][:], func=ACT.Tanh)
+            t_c = acts.tile([P, size, H], F32, name="t_c")
+            nc.scalar.activation(out=t_c[:], in_=x["c"][:], func=ACT.Tanh)
+            not_o = acts.tile([P, size, H], F32, name="not_o")
+            nc.scalar.activation(
+                out=not_o[:], in_=x["iou"][:, :, H : 2 * H], func=ACT.Sigmoid, scale=-1.0
+            )
+            tanh_t = acts.tile([P, size, H], F32, name="tanh_t")
+            nc.scalar.activation(out=tanh_t[:], in_=u_t[:], func=ACT.Tanh)
+            t_u = psum_u.tile([P, size, H], F32, name="t_u")
+            for t in range(size):
+                for blk in range(H_BLOCKS):
+                    cols = slice(blk * P, (blk + 1) * P)
+                    nc.tensor.transpose(t_u[:, t, cols], tanh_t[:, t, cols], ident_f[:])
             th2 = acts.tile([P, 2, size, H], F32, name="th2")
-            nc.scalar.activation(out=th2[:, 1], in_=th[:, 1], func=ACT.Square)
-            nc.scalar.activation(out=th[:, 0], in_=x["iou"][:, :, 2 * H : 3 * H], func=ACT.Tanh)
-            nc.scalar.activation(out=th2[:, 0], in_=th[:, 0], func=ACT.Square)
+            nc.scalar.activation(out=th2[:, 1], in_=t_c[:], func=ACT.Square)
             fc2 = acts.tile([P, size, H], F32, name="fc2")
             nc.scalar.activation(out=fc2[:], in_=x["f"][:], func=ACT.Square, bias=neg_half[:, 0:1])
-            return {"sig": sig, "th": th, "th2": th2, "fc2": fc2}
+            nc.scalar.activation(out=th2[:, 0], in_=t_u[:], func=ACT.Square)
+            return {"sig": sig, "t_c": t_c, "t_u": t_u, "th2": th2, "fc2": fc2, "not_o": not_o}
 
         def children_sum_pe(j):
             mc = inputs[j]["mc"]
@@ -162,7 +182,13 @@ def tile_treelstmcellv2_t_v_kernel(
                 in1=functions[j]["sig"][:, :, H : 2 * H],
                 op=ALU.mult,
             )
-            return {"gh_so": gh_so}
+            if j in VECTOR_SUM_CHUNKS and j < FIRST_GPSIMD_CHUNK:
+                sum_of[j] = children_sum(nc.vector, j)
+            e_o = early.tile([P, size, H], F32, name="e_o")
+            engine.tensor_tensor(
+                out=e_o[:], in0=functions[j]["not_o"][:], in1=functions[j]["t_c"][:], op=ALU.mult
+            )
+            return {"gh_so": gh_so, "e_o": e_o}
 
         def forget_term(j):
             f_term = work.tile([P, CHUNK_SIZES[j], H], F32, name="f_term")
@@ -176,18 +202,23 @@ def tile_treelstmcellv2_t_v_kernel(
             )
             return f_term
 
-        def gradients_first(j):
-            size = CHUNK_SIZES[j]
-            fn = functions[j]
-            e_o = work.tile([P, size, H], F32, name="e_o")
+        def input_term(j):
+            e_i = work.tile([P, CHUNK_SIZES[j], H], F32, name="e_i")
             nc.vector.scalar_tensor_tensor(
-                out=e_o[:],
-                in0=fn["sig"][:, :, H : 2 * H],
+                out=e_i[:],
+                in0=functions[j]["sig"][:, :, 0:H],
                 scalar=1.0,
-                in1=fn["th"][:, 1],
+                in1=functions[j]["t_u"][:],
                 op0=ALU.subtract,
                 op1=ALU.mult,
             )
+            return e_i
+
+        def gradients_first(j):
+            size = CHUNK_SIZES[j]
+            fn = functions[j]
+            if j in VECTOR_SUM_CHUNKS and j >= FIRST_GPSIMD_CHUNK:
+                sum_of[j] = children_sum(nc.vector, j)
             x_neg = work.tile([P, size, H], F32, name="x_neg")
             nc.vector.scalar_tensor_tensor(
                 out=x_neg[:],
@@ -197,7 +228,7 @@ def tile_treelstmcellv2_t_v_kernel(
                 op0=ALU.subtract,
                 op1=ALU.mult,
             )
-            return {"x_neg": x_neg, "e_o": e_o}
+            return {"x_neg": x_neg}
 
         def gradients_rest(j):
             size = CHUNK_SIZES[j]
@@ -213,24 +244,17 @@ def tile_treelstmcellv2_t_v_kernel(
             nc.vector.tensor_tensor(
                 out=dc_neg[:], in0=first_of[j]["x_neg"][:], in1=x["grad"][:, :, H : 2 * H], op=ALU.subtract
             )
-            e_i = work.tile([P, size, H], F32, name="e_i")
-            nc.vector.scalar_tensor_tensor(
-                out=e_i[:],
-                in0=fn["sig"][:, :, 0:H],
-                scalar=1.0,
-                in1=fn["th"][:, 0],
-                op0=ALU.subtract,
-                op1=ALU.mult,
-            )
             if j not in PE_SUM_CHUNKS:
                 term_of[j] = forget_term(j)
+            if j >= 1:
+                quantised[j - 1] = quantise(j - 1)
             dc_si_neg = work.tile([P, size, H], F32, name="dc_si_neg")
             nc.vector.tensor_tensor(out=dc_si_neg[:], in0=dc_neg[:], in1=s_i, op=ALU.mult)
             nc.vector.tensor_tensor(
                 out=dz[:, :, 3 * H : 4 * H], in0=term_of[j][:], in1=dc_neg[:], op=ALU.mult
             )
             nc.vector.tensor_tensor(
-                out=dz[:, :, 0:H], in0=e_i[:], in1=dc_si_neg[:], op=ALU.mult
+                out=dz[:, :, 0:H], in0=input_of[j][:], in1=dc_si_neg[:], op=ALU.mult
             )
             nc.vector.scalar_tensor_tensor(
                 out=dz[:, :, 2 * H : 3 * H],
@@ -243,13 +267,11 @@ def tile_treelstmcellv2_t_v_kernel(
             return {"dz": dz, "diff": diff}
 
         def output_gate(j):
-            nc.vector.scalar_tensor_tensor(
+            nc.vector.tensor_tensor(
                 out=gradients[j]["dz"][:, :, H : 2 * H],
-                in0=first_of[j]["e_o"][:],
-                scalar=-1.0,
+                in0=early_of[j]["e_o"][:],
                 in1=early_of[j]["gh_so"][:],
-                op0=ALU.mult,
-                op1=ALU.mult,
+                op=ALU.mult,
             )
 
         def child_sign(j):
@@ -293,9 +315,6 @@ def tile_treelstmcellv2_t_v_kernel(
             codes = quantised[j]["codes"]
             scales = quantised[j]["scales"]
             dhc = psum_o.tile([P, N_OUT], F32, name="dhc")
-            both = None
-            if j not in LEAN_CHUNKS:
-                both = psum_o.tile([P, N_OUT], F32, name="both")
 
             def one_pass(acc, g, w_from, start, stop):
                 nodes = slice((t * PASSES + g) * P, (t * PASSES + g + 1) * P)
@@ -303,8 +322,8 @@ def tile_treelstmcellv2_t_v_kernel(
                     out=acc[:],
                     lhsT=codes[:, nodes].bitcast(E5M2X4),
                     lhsT_scale=scales[:, nodes],
-                    rhs=w_codes[:, g * N_OUT + w_from : (g + 1) * N_OUT + w_from].bitcast(E4M3X4),
-                    rhs_scale=w_scales[:, g * N_OUT + w_from : (g + 1) * N_OUT + w_from],
+                    rhs=w_codes[:, g, w_from : w_from + N_OUT].bitcast(E4M3X4),
+                    rhs_scale=w_scales[:, g, w_from : w_from + N_OUT],
                     start=start,
                     stop=stop,
                 )
@@ -312,21 +331,24 @@ def tile_treelstmcellv2_t_v_kernel(
             for g in range(PASSES):
                 first = g == 0
                 last = g == PASSES - 1
-                one_pass(dhc, g, 0, first, last)
-                if j not in LEAN_CHUNKS:
-                    one_pass(both, g, 0, first, False)
-                    one_pass(both, g, H, False, last)
-            return {"dhc": dhc, "both": both}
+                if j in LEAN_CHUNKS:
+                    one_pass(dhc, g, 0, first, last)
+                else:
+                    one_pass(dhc, g, 0, first, False)
+                    one_pass(dhc, g, 0, False, False)
+                    one_pass(dhc, g, H, False, last)
+            return {"dhc": dhc}
 
         def shared_part(j):
+            lean = j in LEAN_CHUNKS
             part = results.tile([P, CHUNK_SIZES[j], H], F32, name="part")
             for t in range(CHUNK_SIZES[j]):
                 nc.vector.scalar_tensor_tensor(
                     out=part[:, t],
                     in0=sign_of[j][:, t],
-                    scalar=1.0,
+                    scalar=1.0 if lean else 0.25,
                     in1=products[j, t]["dhc"][:, H : 2 * H],
-                    op0=ALU.add,
+                    op0=ALU.add if lean else ALU.mult,
                     op1=ALU.mult,
                 )
             return part
@@ -346,29 +368,28 @@ def tile_treelstmcellv2_t_v_kernel(
 
         def finish(j, t):
             o_sb = stores.tile([P, 2, H], F32, name="o_sb")
-            nc.vector.scalar_tensor_tensor(
-                out=o_sb[:, 0, :],
-                in0=part_of[j][:, t],
-                scalar=0.5,
-                in1=products[j, t]["dhc"][:, 0:H],
-                op0=ALU.mult,
-                op1=ALU.add,
-            )
-            lean = j in LEAN_CHUNKS
-            nc.vector.scalar_tensor_tensor(
-                out=o_sb[:, 1, :],
-                in0=(other_of[j] if lean else part_of[j])[:, t],
-                scalar=-0.5,
-                in1=products[j, t]["dhc" if lean else "both"][:, 0:H],
-                op0=ALU.mult,
-                op1=ALU.add,
-            )
+            first_half = products[j, t]["dhc"][:, 0:H]
+            if j in LEAN_CHUNKS:
+                nc.vector.scalar_tensor_tensor(
+                    out=o_sb[:, 0, :], in0=part_of[j][:, t], scalar=0.5, in1=first_half, op0=ALU.mult, op1=ALU.add
+                )
+                nc.vector.scalar_tensor_tensor(
+                    out=o_sb[:, 1, :], in0=other_of[j][:, t], scalar=-0.5, in1=first_half, op0=ALU.mult, op1=ALU.add
+                )
+            else:
+                nc.vector.scalar_tensor_tensor(
+                    out=o_sb[:, 0, :], in0=first_half, scalar=0.5, in1=part_of[j][:, t], op0=ALU.mult, op1=ALU.add
+                )
+                nc.vector.scalar_tensor_tensor(
+                    out=o_sb[:, 1, :], in0=first_half, scalar=0.5, in1=part_of[j][:, t], op0=ALU.mult, op1=ALU.subtract
+                )
             nc.sync.dma_start(out=out_v[:, first_group[j] + t], in_=o_sb[:])
 
         functions = {}
         sum_of = {}
         early_of = {}
         term_of = {}
+        input_of = {}
         first_of = {}
         gradients = {}
         sign_of = {}
@@ -384,16 +405,16 @@ def tile_treelstmcellv2_t_v_kernel(
                 if nxt in PE_SUM_CHUNKS:
                     sum_of[nxt] = children_sum_pe(nxt)
             if 0 <= j < CHUNKS:
-                if j in VECTOR_SUM_CHUNKS:
-                    sum_of[j] = children_sum(nc.vector, j)
                 first_of[j] = gradients_first(j)
                 gradients[j] = gradients_rest(j)
-            if 1 <= j <= CHUNKS:
+            if j == CHUNKS:
                 quantised[j - 1] = quantise(j - 1)
             if 0 <= j < CHUNKS:
                 output_gate(j)
                 sign_of[j] = child_sign(j)
                 grouped_dz[j] = transpose_dz(j)
+            if 1 <= j <= CHUNKS:
+                products[j - 1, 0] = multiply(j - 1, 0)
             if 0 <= j and j + LOADS_AHEAD < CHUNKS:
                 inputs[j + LOADS_AHEAD] = load(j + LOADS_AHEAD)
             if nxt < CHUNKS:
@@ -401,6 +422,8 @@ def tile_treelstmcellv2_t_v_kernel(
                 early_of[nxt] = early_results(engine, nxt)
                 if nxt not in PE_SUM_CHUNKS and nxt not in VECTOR_SUM_CHUNKS:
                     sum_of[nxt] = children_sum(nc.gpsimd, nxt)
+            if nxt < CHUNKS:
+                input_of[nxt] = input_term(nxt)
             if j >= 2:
                 part_of[j - 2] = shared_part(j - 2)
                 if j - 2 in LEAN_CHUNKS:
@@ -408,7 +431,7 @@ def tile_treelstmcellv2_t_v_kernel(
             for t in range(GROUPS_PER_CHUNK):
                 if j >= 2 and t < CHUNK_SIZES[j - 2]:
                     finish(j - 2, t)
-                if 1 <= j <= CHUNKS and t < CHUNK_SIZES[j - 1]:
-                    products[j - 1, t] = multiply(j - 1, t)
+                if t == 0 and 1 <= j <= CHUNKS and CHUNK_SIZES[j - 1] > 1:
+                    products[j - 1, 1] = multiply(j - 1, 1)
             if nxt in PE_SUM_CHUNKS:
                 term_of[nxt] = forget_term(nxt)

@@ -56,7 +56,6 @@ def tile_treelstmcellv2_t_v_kernel(
     out_v = out.rearrange("(p s) child h -> p s child h", s=GROUPS)
 
     with ExitStack() as ctx:
-        ctx.enter_context(tc.manual_schedule())
         const = ctx.enter_context(tc.tile_pool(name="const", bufs=1))
         loads = ctx.enter_context(tc.tile_pool(name="loads", bufs=LOADS_AHEAD))
         acts = ctx.enter_context(tc.tile_pool(name="acts", bufs=2))

from contextlib import ExitStack

import concourse.mybir as mybir
from concourse.masks import make_identity

F32 = mybir.dt.float32
BF16 = mybir.dt.bfloat16
U32 = mybir.dt.uint32
U8 = mybir.dt.uint8
I32 = mybir.dt.int32
E4M3X4 = mybir.dt.float8_e4m3fn_x4
E5M2X4 = mybir.dt.float8_e5m2_x4
ALU = mybir.AluOpType
ACT = mybir.ActivationFunctionType

P = 128
PACK = 4
PAIR = 2
GATES = 4
NODES = 2048
H = 256
K = 4 * H
N_OUT = 2 * H
PASSES = K // (P * PACK)
K_BLOCKS = K // P
H_BLOCKS = H // P
IOU_BLOCKS = 3 * H // P
COPY_RUN = 4
GROUPS = NODES // P
GROUPS_PER_CHUNK = 2
CHUNK_SIZES = [GROUPS_PER_CHUNK] * (GROUPS // GROUPS_PER_CHUNK - 1) + [1] * GROUPS_PER_CHUNK
CHUNKS = len(CHUNK_SIZES)
LOADS_AHEAD = 3
FIRST_GPSIMD_CHUNK = 3
PE_SUM_CHUNKS = (1, 2, 3, 4, 5, 6)
VECTOR_SUM_CHUNKS = (0, 7, 8)
GATES_EARLY = (0, 2, 3)
GATES_LATE = (1,)
LEAN_CHUNKS = (7, 8)

FLOPS = 2 * NODES * K * N_OUT


def tile_treelstmcellv2_t_v_kernel(
    tc, mailbox_h, mailbox_c, U_iou_w, b_iou, U_f_w, U_f_b, iou, f, c, grad_out, out
):
    nc = tc.nc
    first_group = [sum(CHUNK_SIZES[:j]) for j in range(CHUNKS)]

    iou_v = iou.rearrange("(p s) z -> p s z", s=GROUPS)
    f_v = f.rearrange("(p s) h -> p s h", s=GROUPS)
    c_v = c.rearrange("(p s) h -> p s h", s=GROUPS)
    grad_v = grad_out.rearrange("(p s) y -> p s y", s=GROUPS)
    mh_v = mailbox_h.rearrange("(p s) child h -> p s child h", s=GROUPS)
    mc_v = mailbox_c.rearrange("(p s) child h -> p s child h", s=GROUPS)
    out_v = out.rearrange("(p s) child h -> p s child h", s=GROUPS)

    with ExitStack() as ctx:
        const = ctx.enter_context(tc.tile_pool(name="const", bufs=1))
        loads = ctx.enter_context(tc.tile_pool(name="loads", bufs=LOADS_AHEAD))
        acts = ctx.enter_context(tc.tile_pool(name="acts", bufs=2))
        work = ctx.enter_context(tc.tile_pool(name="work", bufs=2))
        mx = ctx.enter_context(tc.tile_pool(name="mx", bufs=2))
        results = ctx.enter_context(tc.tile_pool(name="results", bufs=2))
        signs = ctx.enter_context(tc.tile_pool(name="signs", bufs=3))
        early = ctx.enter_context(tc.tile_pool(name="early", bufs=1))
        stores = ctx.enter_context(tc.tile_pool(name="stores", bufs=4))
        psum_t = ctx.enter_context(tc.psum_pool(name="psum_t", bufs=2))
        psum_m = ctx.enter_context(tc.psum_pool(name="psum_m", bufs=1))
        psum_u = ctx.enter_context(tc.psum_pool(name="psum_u", bufs=1))
        psum_o = ctx.enter_context(tc.psum_pool(name="psum_o", bufs=3))

        w_rows = const.tile([P, K_BLOCKS, N_OUT], BF16, name="w_rows")
        w_pairs = w_rows[:].rearrange("p (b e) n -> p b (e n)", e=PAIR)
        iou_w_v = U_iou_w.rearrange("(b p e) n -> p b (e n)", p=P, e=PAIR)
        f_w_v = U_f_w.rearrange("(b p e) n -> p b (e n)", p=P, e=PAIR)
        nc.sync.dma_start(out=w_pairs[:, 0:2, :], in_=iou_w_v[:, 0:2, :])
        nc.sync.dma_start(out=w_pairs[:, 2:3, :], in_=iou_w_v[:, 2:3, :])
        nc.sync.dma_start(out=w_pairs[:, 3:4, :], in_=f_w_v)

        def load(j):
            size = CHUNK_SIZES[j]
            groups = slice(first_group[j], first_group[j] + size)
            iou_sb = loads.tile([P, size, 3 * H], F32, name="iou_sb")
            nc.sync.dma_start(out=iou_sb[:], in_=iou_v[:, groups, :])
            grad_sb = loads.tile([P, size, 2 * H], BF16, name="grad_sb")
            nc.sync.dma_start(out=grad_sb[:], in_=grad_v[:, groups, :])
            c_sb = loads.tile([P, size, H], F32, name="c_sb")
            nc.sync.dma_start(out=c_sb[:], in_=c_v[:, groups, :])
            mc_sb = loads.tile([P, size, 2, H], BF16, name="mc_sb")
            nc.sync.dma_start(out=mc_sb[:], in_=mc_v[:, groups, :, :])
            f_sb = loads.tile([P, size, H], F32, name="f_sb")
            nc.sync.dma_start(out=f_sb[:], in_=f_v[:, groups, :])
            mh_sb = loads.tile([P, size, 2, H], BF16, name="mh_sb")
            nc.sync.dma_start(out=mh_sb[:], in_=mh_v[:, groups, :, :])
            return {"iou": iou_sb, "grad": grad_sb, "c": c_sb, "mc": mc_sb, "f": f_sb, "mh": mh_sb}

        inputs = {}
        for j in range(LOADS_AHEAD):
            inputs[j] = load(j)

        ident = const.tile([P, P], BF16, name="ident")
        make_identity(nc, ident[:])
        ident_f = const.tile([P, P], F32, name="ident_f")
        make_identity(nc, ident_f[:])
        neg_half = const.tile([P, 1], F32, name="neg_half")
        nc.vector.memset(neg_half[:], -0.5)

        w_grouped = const.tile([P, PASSES, N_OUT, PACK], BF16, name="w_grouped", align_bytes=64)
        w_codes = const.tile([P, PASSES, N_OUT + H], U32, name="w_codes", align_bytes=64)
        w_scales = const.tile([P, PASSES, N_OUT + H], U8, name="w_scales", align_bytes=64)
        for g in range(PASSES):
            nc.vector.memset(w_codes[:, g, N_OUT:].bitcast(I32), 0)
            nc.vector.memset(w_scales[:, g, N_OUT:].bitcast(I32), 0)
        for g in range(PASSES):
            nc.vector.tensor_copy(
                out=w_grouped[:, g].rearrange("p (run i) v -> p run v i", i=COPY_RUN),
                in_=w_rows[:, PACK * g : PACK * (g + 1), :].rearrange(
                    "p v (run i) -> p run v i", i=COPY_RUN
                ),
            )
        for g in range(PASSES):
            nc.vector.quantize_mx(
                out=w_codes[:, g, 0:N_OUT].bitcast(E4M3X4),
                scales=w_scales[:, g, 0:N_OUT],
                in_=w_grouped[:, g].rearrange("p n v -> p (n v)"),
            )

        def activations(j):
            size = CHUNK_SIZES[j]
            x = inputs[j]
            u_t = psum_u.tile([P, size, H], F32, name="u_t")
            for t in range(size):
                for blk in range(H_BLOCKS):
                    cols = slice(blk * P, (blk + 1) * P)
                    nc.tensor.transpose(
                        u_t[:, t, cols], x["iou"][:, t, 2 * H + blk * P : 2 * H + (blk + 1) * P], ident_f[:]
                    )
            sig = acts.tile([P, size, 2 * H], F32, name="sig")
            nc.scalar.activation(out=sig[:], in_=x["iou"][:, :, 0 : 2 * H], func=ACT.Sigmoid)
            t_c = acts.tile([P, size, H], F32, name="t_c")
            nc.scalar.activation(out=t_c[:], in_=x["c"][:], func=ACT.Tanh)
            not_o = acts.tile([P, size, H], F32, name="not_o")
            nc.scalar.activation(
                out=not_o[:], in_=x["iou"][:, :, H : 2 * H], func=ACT.Sigmoid, scale=-1.0
            )
            tanh_t = acts.tile([P, size, H], F32, name="tanh_t")
            nc.scalar.activation(out=tanh_t[:], in_=u_t[:], func=ACT.Tanh)
            t_u = psum_u.tile([P, size, H], F32, name="t_u")
            for t in range(size):
                for blk in range(H_BLOCKS):
                    cols = slice(blk * P, (blk + 1) * P)
                    nc.tensor.transpose(t_u[:, t, cols], tanh_t[:, t, cols], ident_f[:])
            th2 = acts.tile([P, 2, size, H], F32, name="th2")
            nc.scalar.activation(out=th2[:, 1], in_=t_c[:], func=ACT.Square)
            fc2 = acts.tile([P, size, H], F32, name="fc2")
            nc.scalar.activation(out=fc2[:], in_=x["f"][:], func=ACT.Square, bias=neg_half[:, 0:1])
            nc.scalar.activation(out=th2[:, 0], in_=t_u[:], func=ACT.Square)
            return {"sig": sig, "t_c": t_c, "t_u": t_u, "th2": th2, "fc2": fc2, "not_o": not_o}

        def children_sum_pe(j):
            mc = inputs[j]["mc"]
            mcs = psum_m.tile([P, CHUNK_SIZES[j], H], F32, name="mcs_ps")
            for t in range(CHUNK_SIZES[j]):
                nc.tensor.matmul(out=mcs[:, t, :], lhsT=ident[:], rhs=mc[:, t, 0, :], start=True, stop=False)
                nc.tensor.matmul(out=mcs[:, t, :], lhsT=ident[:], rhs=mc[:, t, 1, :], start=False, stop=True)
            return mcs

        def children_sum(engine, j):
            mc = inputs[j]["mc"]
            mcs = early.tile([P, CHUNK_SIZES[j], H], F32, name="mcs")
            engine.tensor_tensor(out=mcs[:], in0=mc[:, :, 0, :], in1=mc[:, :, 1, :], op=ALU.add)
            return mcs

        def early_results(engine, j):
            size = CHUNK_SIZES[j]
            gh_so = early.tile([P, size, H], F32, name="gh_so")
            engine.tensor_tensor(
                out=gh_so[:],
                in0=inputs[j]["grad"][:, :, 0:H],
                in1=functions[j]["sig"][:, :, H : 2 * H],
                op=ALU.mult,
            )
            if j in VECTOR_SUM_CHUNKS and j < FIRST_GPSIMD_CHUNK:
                sum_of[j] = children_sum(nc.vector, j)
            e_o = early.tile([P, size, H], F32, name="e_o")
            engine.tensor_tensor(
                out=e_o[:], in0=functions[j]["not_o"][:], in1=functions[j]["t_c"][:], op=ALU.mult
            )
            return {"gh_so": gh_so, "e_o": e_o}

        def forget_term(j):
            f_term = work.tile([P, CHUNK_SIZES[j], H], F32, name="f_term")
            nc.vector.scalar_tensor_tensor(
                out=f_term[:],
                in0=functions[j]["fc2"][:],
                scalar=0.25,
                in1=sum_of[j][:],
                op0=ALU.subtract,
                op1=ALU.mult,
            )
            return f_term

        def input_term(j):
            e_i = work.tile([P, CHUNK_SIZES[j], H], F32, name="e_i")
            nc.vector.scalar_tensor_tensor(
                out=e_i[:],
                in0=functions[j]["sig"][:, :, 0:H],
                scalar=1.0,
                in1=functions[j]["t_u"][:],
                op0=ALU.subtract,
                op1=ALU.mult,
            )
            return e_i

        def gradients_first(j):
            size = CHUNK_SIZES[j]
            fn = functions[j]
            if j in VECTOR_SUM_CHUNKS and j >= FIRST_GPSIMD_CHUNK:
                sum_of[j] = children_sum(nc.vector, j)
            x_neg = work.tile([P, size, H], F32, name="x_neg")
            nc.vector.scalar_tensor_tensor(
                out=x_neg[:],
                in0=fn["th2"][:, 1],
                scalar=1.0,
                in1=early_of[j]["gh_so"][:],
                op0=ALU.subtract,
                op1=ALU.mult,
            )
            return {"x_neg": x_neg}

        def gradients_rest(j):
            size = CHUNK_SIZES[j]
            x = inputs[j]
            fn = functions[j]
            s_i = fn["sig"][:, :, 0:H]
            dz = mx.tile([P, size, K], BF16, name="dz")
            diff = signs.tile([P, size, H], BF16, name="diff")
            nc.vector.tensor_tensor(
                out=diff[:], in0=x["mh"][:, :, 0, :], in1=x["mh"][:, :, 1, :], op=ALU.subtract
            )
            dc_neg = work.tile([P, size, H], F32, name="dc_neg")
            nc.vector.tensor_tensor(
                out=dc_neg[:], in0=first_of[j]["x_neg"][:], in1=x["grad"][:, :, H : 2 * H], op=ALU.subtract
            )
            if j not in PE_SUM_CHUNKS:
                term_of[j] = forget_term(j)
            if j >= 1:
                quantised[j - 1] = quantise(j - 1)
            dc_si_neg = work.tile([P, size, H], F32, name="dc_si_neg")
            nc.vector.tensor_tensor(out=dc_si_neg[:], in0=dc_neg[:], in1=s_i, op=ALU.mult)
            nc.vector.tensor_tensor(
                out=dz[:, :, 3 * H : 4 * H], in0=term_of[j][:], in1=dc_neg[:], op=ALU.mult
            )
            nc.vector.tensor_tensor(
                out=dz[:, :, 0:H], in0=input_of[j][:], in1=dc_si_neg[:], op=ALU.mult
            )
            nc.vector.scalar_tensor_tensor(
                out=dz[:, :, 2 * H : 3 * H],
                in0=fn["th2"][:, 0],
                scalar=1.0,
                in1=dc_si_neg[:],
                op0=ALU.subtract,
                op1=ALU.mult,
            )
            return {"dz": dz, "diff": diff}

        def output_gate(j):
            nc.vector.tensor_tensor(
                out=gradients[j]["dz"][:, :, H : 2 * H],
                in0=early_of[j]["e_o"][:],
                in1=early_of[j]["gh_so"][:],
                op=ALU.mult,
            )

        def child_sign(j):
            sgn = signs.tile([P, CHUNK_SIZES[j], H], BF16, name="sgn")
            nc.scalar.activation(out=sgn[:], in_=gradients[j]["diff"][:], func=ACT.Sign)
            return sgn

        def transpose_dz(j):
            size = CHUNK_SIZES[j]
            dz = gradients[j]["dz"]
            grouped = mx.tile([P, size * K], BF16, name="grouped", align_bytes=64)
            banks = []
            for t in range(size):
                words = dz[:, t, :].bitcast(F32)
                dz_t = psum_t.tile([P, GATES, P], F32, name="dz_t")
                banks.append(dz_t)
                for b in GATES_EARLY:
                    nc.tensor.transpose(dz_t[:, b, :], words[:, b * P : (b + 1) * P], ident_f[:])
            for t in range(size):
                words = dz[:, t, :].bitcast(F32)
                for b in GATES_LATE:
                    nc.tensor.transpose(banks[t][:, b, :], words[:, b * P : (b + 1) * P], ident_f[:])
                nc.scalar.copy(
                    out=grouped[:, t * K : (t + 1) * K]
                    .bitcast(F32)
                    .rearrange("p (g node u) -> p g node u", g=PASSES, u=PAIR),
                    in_=banks[t][:].rearrange("p (g u) node -> p g node u", u=PAIR),
                )
            return grouped

        def quantise(j):
            size = CHUNK_SIZES[j]
            codes = mx.tile([P, size * PASSES * P], U32, name="codes", align_bytes=64)
            scales = mx.tile([P, size * PASSES * P], U8, name="scales", align_bytes=64)
            nc.vector.quantize_mx(
                out=codes[:].bitcast(E5M2X4), scales=scales[:], in_=grouped_dz[j][:]
            )
            return {"codes": codes, "scales": scales}

        def multiply(j, t):
            codes = quantised[j]["codes"]
            scales = quantised[j]["scales"]
            dhc = psum_o.tile([P, N_OUT], F32, name="dhc")

            def one_pass(acc, g, w_from, start, stop):
                nodes = slice((t * PASSES + g) * P, (t * PASSES + g + 1) * P)
                nc.tensor.matmul_mx(
                    out=acc[:],
                    lhsT=codes[:, nodes].bitcast(E5M2X4),
                    lhsT_scale=scales[:, nodes],
                    rhs=w_codes[:, g, w_from : w_from + N_OUT].bitcast(E4M3X4),
                    rhs_scale=w_scales[:, g, w_from : w_from + N_OUT],
                    start=start,
                    stop=stop,
                )

            for g in range(PASSES):
                first = g == 0
                last = g == PASSES - 1
                if j in LEAN_CHUNKS:
                    one_pass(dhc, g, 0, first, last)
                else:
                    one_pass(dhc, g, 0, first, False)
                    one_pass(dhc, g, 0, False, False)
                    one_pass(dhc, g, H, False, last)
            return {"dhc": dhc}

        def shared_part(j):
            lean = j in LEAN_CHUNKS
            part = results.tile([P, CHUNK_SIZES[j], H], F32, name="part")
            for t in range(CHUNK_SIZES[j]):
                nc.vector.scalar_tensor_tensor(
                    out=part[:, t],
                    in0=sign_of[j][:, t],
                    scalar=1.0 if lean else 0.25,
                    in1=products[j, t]["dhc"][:, H : 2 * H],
                    op0=ALU.add if lean else ALU.mult,
                    op1=ALU.mult,
                )
            return part

        def other_part(j):
            other = results.tile([P, CHUNK_SIZES[j], H], F32, name="other")
            for t in range(CHUNK_SIZES[j]):
                nc.vector.scalar_tensor_tensor(
                    out=other[:, t],
                    in0=sign_of[j][:, t],
                    scalar=1.0,
                    in1=products[j, t]["dhc"][:, H : 2 * H],
                    op0=ALU.subtract,
                    op1=ALU.mult,
                )
            return other

        def finish(j, t):
            o_sb = stores.tile([P, 2, H], F32, name="o_sb")
            first_half = products[j, t]["dhc"][:, 0:H]
            if j in LEAN_CHUNKS:
                nc.vector.scalar_tensor_tensor(
                    out=o_sb[:, 0, :], in0=part_of[j][:, t], scalar=0.5, in1=first_half, op0=ALU.mult, op1=ALU.add
                )
                nc.vector.scalar_tensor_tensor(
                    out=o_sb[:, 1, :], in0=other_of[j][:, t], scalar=-0.5, in1=first_half, op0=ALU.mult, op1=ALU.add
                )
            else:
                nc.vector.scalar_tensor_tensor(
                    out=o_sb[:, 0, :], in0=first_half, scalar=0.5, in1=part_of[j][:, t], op0=ALU.mult, op1=ALU.add
                )
                nc.vector.scalar_tensor_tensor(
                    out=o_sb[:, 1, :], in0=first_half, scalar=0.5, in1=part_of[j][:, t], op0=ALU.mult, op1=ALU.subtract
                )
            nc.sync.dma_start(out=out_v[:, first_group[j] + t], in_=o_sb[:])

        functions = {}
        sum_of = {}
        early_of = {}
        term_of = {}
        input_of = {}
        first_of = {}
        gradients = {}
        sign_of = {}
        grouped_dz = {}
        quantised = {}
        products = {}
        part_of = {}
        other_of = {}
        for j in range(-1, CHUNKS + 2):
            nxt = j + 1
            if nxt < CHUNKS:
                functions[nxt] = activations(nxt)
                if nxt in PE_SUM_CHUNKS:
                    sum_of[nxt] = children_sum_pe(nxt)
            if 0 <= j < CHUNKS:
                first_of[j] = gradients_first(j)
                gradients[j] = gradients_rest(j)
            if j == CHUNKS:
                quantised[j - 1] = quantise(j - 1)
            if 0 <= j < CHUNKS:
                output_gate(j)
                sign_of[j] = child_sign(j)
                grouped_dz[j] = transpose_dz(j)
            if 1 <= j <= CHUNKS:
                products[j - 1, 0] = multiply(j - 1, 0)
            if 0 <= j and j + LOADS_AHEAD < CHUNKS:
                inputs[j + LOADS_AHEAD] = load(j + LOADS_AHEAD)
            if nxt < CHUNKS:
                engine = nc.gpsimd if nxt >= FIRST_GPSIMD_CHUNK else nc.vector
                early_of[nxt] = early_results(engine, nxt)
                if nxt not in PE_SUM_CHUNKS and nxt not in VECTOR_SUM_CHUNKS:
                    sum_of[nxt] = children_sum(nc.gpsimd, nxt)
            if nxt < CHUNKS:
                input_of[nxt] = input_term(nxt)
            if j >= 2:
                part_of[j - 2] = shared_part(j - 2)
                if j - 2 in LEAN_CHUNKS:
                    other_of[j - 2] = other_part(j - 2)
            for t in range(GROUPS_PER_CHUNK):
                if j >= 2 and t < CHUNK_SIZES[j - 2]:
                    finish(j - 2, t)
                if t == 0 and 1 <= j <= CHUNKS and CHUNK_SIZES[j - 1] > 1:
                    products[j - 1, 1] = multiply(j - 1, 1)
            if nxt in PE_SUM_CHUNKS:
                term_of[nxt] = forget_term(nxt)
